import numpy as np
import ml_dtypes


def mxq(x, axis, fmt="e4m3"):
    dtype, down = {"e4m3": (ml_dtypes.float8_e4m3fn, 7), "e5m2": (ml_dtypes.float8_e5m2, 14)}[fmt]
    v = np.moveaxis(np.asarray(x, np.float32).astype(ml_dtypes.bfloat16).astype(np.float64), axis, -1)
    blocks = v.reshape(v.shape[:-1] + (-1, 32))
    amax = np.abs(blocks).max(-1, keepdims=True)
    byte = np.maximum(np.where(amax > 0, np.frexp(amax)[1] - 1 + 127, 0) - down, 1)
    scale = np.exp2(byte - 127.0)
    codes = (blocks / scale).astype(np.float32).astype(dtype).astype(np.float64)
    return np.moveaxis((codes * scale).reshape(v.shape), -1, axis)


WIDE = False


def mx_kscale(k):
    if not WIDE:
        return np.ones(k)
    levels = np.array([10, -10, 5, -5, 0])
    a = np.random.permutation(np.resize(levels, k // 512 * 4)).reshape(k // 512, 4)
    idx = np.arange(k)
    return np.exp2(a[idx // 512, idx % 128 // 32])


BF16 = ml_dtypes.bfloat16


def bf(x):
    return np.asarray(x, np.float32).astype(BF16)


def f64(x):
    return np.asarray(x).astype(np.float64)


L, F, O, N, B, D = 2, 512, 512, 1024, 1, 3
G = O + O + O


def sigmoid(v):
    return 1.0 / (1.0 + np.exp(-v))


def setup_inputs():
    s = mx_kscale(O)
    return {"agg": bf(np.random.standard_normal((D, B, N, O)) * s),
            "x": bf(np.random.standard_normal((N, B, F))),
            "wih": bf(np.random.standard_normal((G, O)) * 0.7 / np.sqrt(O) / s),
            "whh": bf(np.random.standard_normal((G, O)) * 0.7 / np.sqrt(O)),
            "bih": bf(np.random.standard_normal(G) * 0.3),
            "bhh": bf(np.random.standard_normal(G) * 0.3),
            "wh": bf(np.random.standard_normal((F, O)) * 0.5 / np.sqrt(F)),
            "bh": bf(0.3 + np.random.standard_normal(O) * 0.2)}


def reference(agg, x, wih, whh, bih, bhh, wh, bh):
    x = f64(x)
    xq = mxq(x, 2, "e4m3")
    h = x.transpose(1, 0, 2)[None]
    gi = (mxq(f64(agg), 3, "e4m3") @ mxq(f64(wih), 1, "e4m3").T) + f64(bih)
    gh = (xq.transpose(1, 0, 2)[None] @ mxq(f64(whh), 1, "e4m3").T) + f64(bhh)
    r = sigmoid(gi[..., :O] + gh[..., :O])
    z = sigmoid(gi[..., O:O + O] + gh[..., O:O + O])
    n = np.tanh(gi[..., O + O:] + r * gh[..., O + O:])
    hnew = (1.0 - z) * n + z * h
    upd = np.maximum(hnew.sum(0).transpose(1, 0, 2), 0.0)
    t = np.maximum((xq @ mxq(f64(wh), 0, "e4m3")) + f64(bh), 0.0)
    return upd * t + x * (1.0 - t)

@@ -1,0 +1,252 @@
+from contextlib import ExitStack
+
+import concourse.mybir as mybir
+from concourse.masks import make_identity
+
+F32 = mybir.dt.float32
+BF16 = mybir.dt.bfloat16
+U32 = mybir.dt.uint32
+U8 = mybir.dt.uint8
+FP8X4 = mybir.dt.float8_e4m3fn_x4
+ACT = mybir.ActivationFunctionType
+ALU = mybir.AluOpType
+
+P = 128
+PACK = 4
+K = P * PACK
+DIRS = 3
+NODES = 1024
+FEATS = 512
+NODE_TILES = NODES // P
+FEAT_TILES = FEATS // P
+CHUNK_TILES = 4
+CHUNK = CHUNK_TILES * P
+CHUNKS = NODE_TILES // CHUNK_TILES
+HH_R = 0
+HH_Z = 1
+HH_N = 2
+IH_R = 3
+IH_Z = 4
+IH_N = 5
+
+FLOPS = 2 * K * NODES * (DIRS * 3 * FEATS + 3 * FEATS + FEATS)
+
+
+def tile_graphconvolution_pb_kernel(tc, agg, x, wih, whh, bih, bhh, wh, bh, out):
+    nc = tc.nc
+    with ExitStack() as stack:
+        keep = stack.enter_context(tc.tile_pool(name="keep", bufs=1))
+        stage = stack.enter_context(tc.tile_pool(name="stage", bufs=3))
+        work = stack.enter_context(tc.tile_pool(name="work", bufs=2))
+        psum = stack.enter_context(tc.psum_pool(name="psum", bufs=1))
+
+        x_nat = keep.tile([P, NODE_TILES, FEATS], BF16)
+        agg_nat = keep.tile([P, DIRS, NODE_TILES, FEATS], BF16)
+        w_nat = keep.tile([P, FEAT_TILES, 6, K], BF16)
+        wh_nat = keep.tile([P, PACK, FEATS], BF16)
+        bias_rows = keep.tile([P, P], BF16)
+
+        x_view = x.rearrange("(p t) b f -> p t (b f)", t=NODE_TILES)
+        agg_view = agg.rearrange("d b (p t) f -> d p (b t) f", t=NODE_TILES)
+        out_view = out.rearrange("(p t) b f -> p t (b f)", t=NODE_TILES)
+        whh_view = whh.rearrange("(g f m) k -> f m g k", g=3, f=FEAT_TILES)
+        wih_view = wih.rearrange("(g f m) k -> f m g k", g=3, f=FEAT_TILES)
+
+        def load_x(c):
+            tiles = slice(c * CHUNK_TILES, (c + 1) * CHUNK_TILES)
+            nc.sync.dma_start(out=x_nat[:, tiles, :], in_=x_view[:, tiles, :])
+
+        def load_agg(d, c):
+            tiles = slice(c * CHUNK_TILES, (c + 1) * CHUNK_TILES)
+            nc.sync.dma_start(out=agg_nat[:, d, tiles, :], in_=agg_view[d][:, tiles, :])
+
+        def load_weights(f):
+            nc.sync.dma_start(out=w_nat[:, f, HH_R : HH_N + 1, :], in_=whh_view[f])
+            nc.sync.dma_start(out=w_nat[:, f, IH_R : IH_N + 1, :], in_=wih_view[f])
+
+        nc.vector.memset(bias_rows[:], 0.0)
+        nc.scalar.dma_start(out=bias_rows[0:12, :], in_=bih.rearrange("(r m) -> r m", m=P))
+        nc.scalar.dma_start(out=bias_rows[12:24, :], in_=bhh.rearrange("(r m) -> r m", m=P))
+        nc.scalar.dma_start(out=bias_rows[24:28, :], in_=bh.rearrange("(r m) -> r m", m=P))
+        load_x(0)
+        load_weights(0)
+        load_agg(0, 0)
+        nc.sync.dma_start(
+            out=wh_nat[:].rearrange("p (u e) o -> p u (e o)", u=2),
+            in_=wh.rearrange("(u p e) o -> p u (e o)", u=2, e=2),
+        )
+        load_agg(1, 0)
+        load_agg(2, 0)
+        for f in range(1, FEAT_TILES):
+            load_weights(f)
+        load_x(1)
+        for d in range(DIRS):
+            load_agg(d, 1)
+
+        x_codes = keep.tile([P, NODES], U32, align_bytes=64)
+        x_scales = keep.tile([P, NODES], U8, align_bytes=64)
+        agg_codes = keep.tile([P, DIRS, NODES], U32, align_bytes=64)
+        agg_scales = keep.tile([P, DIRS, NODES], U8, align_bytes=64)
+        w_codes = keep.tile([P, FEAT_TILES, 6, P], U32, align_bytes=64)
+        w_scales = keep.tile([P, FEAT_TILES, 6, P], U8, align_bytes=64)
+        wh_codes = keep.tile([P, FEATS], U32, align_bytes=64)
+        wh_scales = keep.tile([P, FEATS], U8, align_bytes=64)
+
+        ident = keep.tile([P, P], F32)
+        make_identity(nc, ident[:])
+
+        def quantise_two_tiles(rows, codes, scales, copy):
+            words = rows.bitcast(F32)
+            flipped = psum.tile([P, 2, 2, P], F32, tag="node", bufs=3)
+            for i in range(2):
+                for u in range(2):
+                    nc.tensor.transpose(flipped[:, i, u, :], words[:, i, u * P : (u + 1) * P], ident[:])
+            grouped = stage.tile([P, 2, P, PACK], BF16, align_bytes=64)
+            copy(out=grouped[:].bitcast(F32), in_=flipped[:].rearrange("p i u r -> p i r u"))
+            nc.vector.quantize_mx(
+                out=codes.bitcast(FP8X4), scales=scales, in_=grouped[:].rearrange("p i r t -> p (i r t)")
+            )
+
+        def quantise_nodes(nat, codes, scales, c, copies):
+            for h in range(CHUNK_TILES // 2):
+                t = c * CHUNK_TILES + 2 * h
+                cols = slice(t * P, (t + 2) * P)
+                quantise_two_tiles(nat[:, t : t + 2, :], codes[:, cols], scales[:, cols], copies[h % len(copies)])
+
+        def quantise_weights(f, copies):
+            for h in range(3):
+                quantise_two_tiles(
+                    w_nat[:, f, 2 * h : 2 * h + 2, :],
+                    w_codes[:, f, 2 * h : 2 * h + 2, :].rearrange("p i m -> p (i m)"),
+                    w_scales[:, f, 2 * h : 2 * h + 2, :].rearrange("p i m -> p (i m)"),
+                    copies[h % len(copies)],
+                )
+
+        both = [nc.scalar.copy, nc.vector.tensor_copy]
+        scalar_only = [nc.scalar.copy]
+
+        bias_rows32 = keep.tile([P, P], F32)
+        nc.vector.tensor_copy(out=bias_rows32[:], in_=bias_rows[:])
+        bias_flipped = psum.tile([P, P], F32, tag="node", bufs=3)
+        nc.tensor.transpose(bias_flipped[:], bias_rows32[:], ident[:])
+        bias_cols = keep.tile([P, 32], F32)
+        nc.vector.tensor_copy(out=bias_cols[:], in_=bias_flipped[:, 0:32])
+        b_r = keep.tile([P, FEAT_TILES], F32)
+        nc.vector.tensor_tensor(out=b_r[:], in0=bias_cols[:, 0:4], in1=bias_cols[:, 12:16], op=ALU.add)
+        minus_b_z = keep.tile([P, FEAT_TILES], F32)
+        nc.vector.scalar_tensor_tensor(
+            out=minus_b_z[:], in0=bias_cols[:, 4:8], scalar=-1.0, in1=bias_cols[:, 16:20],
+            op0=ALU.mult, op1=ALU.subtract,
+        )
+
+        quantise_nodes(x_nat, x_codes, x_scales, 0, both)
+        quantise_weights(0, both)
+        quantise_nodes(agg_nat[:, 0], agg_codes[:, 0], agg_scales[:, 0], 0, both)
+        wh_grouped = stage.tile([P, FEATS, PACK], BF16, align_bytes=64, bufs=1)
+        nc.vector.tensor_copy(out=wh_grouped[:], in_=wh_nat[:].rearrange("p t o -> p o t"))
+        nc.vector.quantize_mx(
+            out=wh_codes[:].bitcast(FP8X4), scales=wh_scales[:], in_=wh_grouped[:].rearrange("p o t -> p (o t)")
+        )
+
+        def weight_pass(acc, f, g, codes, scales, start, stop):
+            nc.tensor.matmul_mx(
+                out=acc[:],
+                lhsT=w_codes[:, f, g, :].bitcast(FP8X4),
+                lhsT_scale=w_scales[:, f, g, :],
+                rhs=codes.bitcast(FP8X4),
+                rhs_scale=scales,
+                start=start,
+                stop=stop,
+            )
+
+        def by_tile(t):
+            return t[:].rearrange("p (j m) -> p j m", j=CHUNK_TILES)
+
+        for c in range(CHUNKS):
+            nodes = slice(c * CHUNK, (c + 1) * CHUNK)
+            xq = (x_codes[:, nodes], x_scales[:, nodes])
+            for f in range(FEAT_TILES):
+                feats = slice(f * P, (f + 1) * P)
+                if c == 0:
+                    if f + 1 < FEAT_TILES:
+                        quantise_weights(f + 1, scalar_only)
+                    if f == 0:
+                        quantise_nodes(x_nat, x_codes, x_scales, 1, scalar_only)
+                    else:
+                        quantise_nodes(agg_nat[:, f - 1], agg_codes[:, f - 1], agg_scales[:, f - 1], 1, scalar_only)
+
+                hid_n = psum.tile([P, CHUNK], F32, tag="hn", bufs=1)
+                weight_pass(hid_n, f, HH_N, xq[0], xq[1], True, True)
+                hw_acc = psum.tile([P, CHUNK], F32, tag="gate", bufs=4)
+                nc.tensor.matmul_mx(
+                    out=hw_acc[:], lhsT=wh_codes[:, feats].bitcast(FP8X4), lhsT_scale=wh_scales[:, feats],
+                    rhs=xq[0].bitcast(FP8X4), rhs_scale=xq[1], start=True, stop=True,
+                )
+                hw = work.tile([P, CHUNK], F32, tag="hw")
+                nc.scalar.activation(out=hw[:], in_=hw_acc[:], func=ACT.Relu, bias=bias_cols[:, 24 + f : 25 + f])
+
+                fresh = []
+                part = []
+                for d in range(DIRS):
+                    if c == 0 and f == 0 and d + 1 < DIRS:
+                        quantise_nodes(agg_nat[:, d + 1], agg_codes[:, d + 1], agg_scales[:, d + 1], 0, scalar_only)
+                    aq = (agg_codes[:, d, nodes], agg_scales[:, d, nodes])
+                    acc_r = psum.tile([P, CHUNK], F32, tag="gate", bufs=4)
+                    weight_pass(acc_r, f, IH_R, aq[0], aq[1], True, False)
+                    weight_pass(acc_r, f, HH_R, xq[0], xq[1], False, True)
+                    acc_z = psum.tile([P, CHUNK], F32, tag="gate", bufs=4)
+                    weight_pass(acc_z, f, IH_Z, aq[0], aq[1], True, False)
+                    weight_pass(acc_z, f, HH_Z, xq[0], xq[1], False, True)
+                    acc_n = psum.tile([P, CHUNK], F32, tag="gate", bufs=4)
+                    weight_pass(acc_n, f, IH_N, aq[0], aq[1], True, True)
+
+                    reset = work.tile([P, CHUNK], F32, tag="reset")
+                    nc.scalar.activation(out=reset[:], in_=acc_r[:], func=ACT.Sigmoid, bias=b_r[:, f : f + 1])
+                    fresh_d = work.tile([P, CHUNK], F32, tag="fresh", bufs=6)
+                    nc.scalar.activation(
+                        out=fresh_d[:], in_=acc_z[:], func=ACT.Sigmoid, bias=minus_b_z[:, f : f + 1], scale=-1.0
+                    )
+                    pre = work.tile([P, CHUNK], F32, tag="pre")
+                    nc.vector.scalar_tensor_tensor(
+                        out=pre[:], in0=hid_n[:], scalar=bias_cols[:, 20 + f : 21 + f], in1=reset[:],
+                        op0=ALU.add, op1=ALU.mult,
+                    )
+                    nc.vector.tensor_tensor(out=pre[:], in0=acc_n[:], in1=pre[:], op=ALU.add)
+                    cand = work.tile([P, CHUNK], F32, tag="cand")
+                    nc.scalar.activation(out=cand[:], in_=pre[:], func=ACT.Tanh, bias=bias_cols[:, 8 + f : 9 + f])
+                    part_d = work.tile([P, CHUNK], F32, tag="part", bufs=6)
+                    nc.vector.tensor_tensor(out=part_d[:], in0=fresh_d[:], in1=cand[:], op=ALU.mult)
+                    fresh.append(fresh_d)
+                    part.append(part_d)
+
+                fresh_sum = psum.tile([P, CHUNK], F32, tag="node", bufs=3)
+                part_sum = psum.tile([P, CHUNK], F32, tag="node", bufs=3)
+                hw_nodes = psum.tile([P, CHUNK], F32, tag="node", bufs=3)
+                for total, terms in ((fresh_sum, fresh), (part_sum, part), (hw_nodes, [hw])):
+                    for j in range(CHUNK_TILES):
+                        cols = slice(j * P, (j + 1) * P)
+                        for i, term in enumerate(terms):
+                            nc.tensor.matmul(
+                                out=total[:, cols], lhsT=term[:, cols], rhs=ident[:], is_transpose=True,
+                                start=(i == 0), stop=(i == len(terms) - 1),
+                            )
+
+                x_blk = x_nat[:, c * CHUNK_TILES : (c + 1) * CHUNK_TILES, feats]
+                minus_zh = work.tile([P, CHUNK], F32, tag="minus_zh")
+                nc.vector.scalar_tensor_tensor(
+                    out=by_tile(minus_zh), in0=by_tile(fresh_sum), scalar=float(DIRS), in1=x_blk,
+                    op0=ALU.subtract, op1=ALU.mult,
+                )
+                hsum = work.tile([P, CHUNK], F32, tag="hsum")
+                nc.vector.tensor_tensor(out=hsum[:], in0=part_sum[:], in1=minus_zh[:], op=ALU.subtract)
+                diff = work.tile([P, CHUNK], F32, tag="diff")
+                nc.vector.scalar_tensor_tensor(
+                    out=by_tile(diff), in0=by_tile(hsum), scalar=0.0, in1=x_blk, op0=ALU.max, op1=ALU.subtract
+                )
+                gated = work.tile([P, CHUNK], F32, tag="gated")
+                nc.vector.tensor_tensor(out=gated[:], in0=hw_nodes[:], in1=diff[:], op=ALU.mult)
+                result = work.tile([P, CHUNK], F32, tag="result", bufs=3)
+                nc.vector.tensor_tensor(out=by_tile(result), in0=by_tile(gated), in1=x_blk, op=ALU.add)
+                nc.sync.dma_start(
+                    out=out_view[:, c * CHUNK_TILES : (c + 1) * CHUNK_TILES, feats], in_=by_tile(result)
+                )

@@ -22,12 +22,21 @@ FEAT_TILES = FEATS // P
 CHUNK_TILES = 4
 CHUNK = CHUNK_TILES * P
 CHUNKS = NODE_TILES // CHUNK_TILES
+BLOCKS = CHUNKS * FEAT_TILES
+STEPS = BLOCKS * DIRS
 HH_R = 0
 HH_Z = 1
 HH_N = 2
 IH_R = 3
 IH_Z = 4
 IH_N = 5
+BIH_R = 0
+BIH_Z = 4
+BIH_N = 8
+BHH_R = 12
+BHH_Z = 16
+BHH_N = 20
+BH = 24
 
 FLOPS = 2 * K * NODES * (DIRS * 3 * FEATS + 3 * FEATS + FEATS)
 
@@ -36,9 +45,9 @@ def tile_graphconvolution_pb_kernel(tc, agg, x, wih, whh, bih, bhh, wh, bh, out)
     nc = tc.nc
     with ExitStack() as stack:
         keep = stack.enter_context(tc.tile_pool(name="keep", bufs=1))
-        stage = stack.enter_context(tc.tile_pool(name="stage", bufs=3))
         work = stack.enter_context(tc.tile_pool(name="work", bufs=2))
         psum = stack.enter_context(tc.psum_pool(name="psum", bufs=1))
+        stack.enter_context(tc.manual_schedule())
 
         x_nat = keep.tile([P, NODE_TILES, FEATS], BF16)
         agg_nat = keep.tile([P, DIRS, NODE_TILES, FEATS], BF16)
@@ -52,31 +61,32 @@ def tile_graphconvolution_pb_kernel(tc, agg, x, wih, whh, bih, bhh, wh, bh, out)
         whh_view = whh.rearrange("(g f m) k -> f m g k", g=3, f=FEAT_TILES)
         wih_view = wih.rearrange("(g f m) k -> f m g k", g=3, f=FEAT_TILES)
 
+        def chunk_tiles(c):
+            return slice(c * CHUNK_TILES, (c + 1) * CHUNK_TILES)
+
         def load_x(c):
-            tiles = slice(c * CHUNK_TILES, (c + 1) * CHUNK_TILES)
-            nc.sync.dma_start(out=x_nat[:, tiles, :], in_=x_view[:, tiles, :])
+            nc.sync.dma_start(out=x_nat[:, chunk_tiles(c), :], in_=x_view[:, chunk_tiles(c), :])
 
         def load_agg(d, c):
-            tiles = slice(c * CHUNK_TILES, (c + 1) * CHUNK_TILES)
-            nc.sync.dma_start(out=agg_nat[:, d, tiles, :], in_=agg_view[d][:, tiles, :])
+            nc.sync.dma_start(out=agg_nat[:, d, chunk_tiles(c), :], in_=agg_view[d][:, chunk_tiles(c), :])
 
         def load_weights(f):
             nc.sync.dma_start(out=w_nat[:, f, HH_R : HH_N + 1, :], in_=whh_view[f])
             nc.sync.dma_start(out=w_nat[:, f, IH_R : IH_N + 1, :], in_=wih_view[f])
 
         nc.vector.memset(bias_rows[:], 0.0)
-        nc.scalar.dma_start(out=bias_rows[0:12, :], in_=bih.rearrange("(r m) -> r m", m=P))
-        nc.scalar.dma_start(out=bias_rows[12:24, :], in_=bhh.rearrange("(r m) -> r m", m=P))
-        nc.scalar.dma_start(out=bias_rows[24:28, :], in_=bh.rearrange("(r m) -> r m", m=P))
+        nc.scalar.dma_start(out=bias_rows[BIH_R:BHH_R, :], in_=bih.rearrange("(r m) -> r m", m=P))
+        nc.scalar.dma_start(out=bias_rows[BHH_R:BH, :], in_=bhh.rearrange("(r m) -> r m", m=P))
+        nc.scalar.dma_start(out=bias_rows[BH : BH + FEAT_TILES, :], in_=bh.rearrange("(r m) -> r m", m=P))
         load_x(0)
-        load_weights(0)
         load_agg(0, 0)
+        load_weights(0)
+        load_agg(1, 0)
+        load_agg(2, 0)
         nc.sync.dma_start(
             out=wh_nat[:].rearrange("p (u e) o -> p u (e o)", u=2),
             in_=wh.rearrange("(u p e) o -> p u (e o)", u=2, e=2),
         )
-        load_agg(1, 0)
-        load_agg(2, 0)
         for f in range(1, FEAT_TILES):
             load_weights(f)
         load_x(1)
@@ -95,35 +105,184 @@ def tile_graphconvolution_pb_kernel(tc, agg, x, wih, whh, bih, bhh, wh, bh, out)
         ident = keep.tile([P, P], F32)
         make_identity(nc, ident[:])
 
-        def quantise_two_tiles(rows, codes, scales, copy):
-            words = rows.bitcast(F32)
+        def node_units(nat, codes, scales, c):
+            units = []
+            for t in range(c * CHUNK_TILES, (c + 1) * CHUNK_TILES, 2):
+                cols = slice(t * P, (t + 2) * P)
+                units.append((nat[:, t : t + 2, :], codes[:, cols], scales[:, cols]))
+            return units
+
+        def weight_units(f):
+            units = []
+            for g in range(0, 6, 2):
+                units.append(
+                    (
+                        w_nat[:, f, g : g + 2, :],
+                        w_codes[:, f, g : g + 2, :].rearrange("p i m -> p (i m)"),
+                        w_scales[:, f, g : g + 2, :].rearrange("p i m -> p (i m)"),
+                    )
+                )
+            return units
+
+        def flip(unit):
+            words = unit[0].bitcast(F32)
             flipped = psum.tile([P, 2, 2, P], F32, tag="node", bufs=3)
             for i in range(2):
                 for u in range(2):
                     nc.tensor.transpose(flipped[:, i, u, :], words[:, i, u * P : (u + 1) * P], ident[:])
-            grouped = stage.tile([P, 2, P, PACK], BF16, align_bytes=64)
+            return flipped
+
+        def regroup(flipped, copy):
+            grouped = work.tile([P, 2, P, PACK], BF16, align_bytes=64, tag="grouped", bufs=6)
             copy(out=grouped[:].bitcast(F32), in_=flipped[:].rearrange("p i u r -> p i r u"))
+            return grouped
+
+        def quantise(unit, grouped):
             nc.vector.quantize_mx(
-                out=codes.bitcast(FP8X4), scales=scales, in_=grouped[:].rearrange("p i r t -> p (i r t)")
+                out=unit[1].bitcast(FP8X4), scales=unit[2], in_=grouped[:].rearrange("p i r t -> p (i r t)")
             )
 
-        def quantise_nodes(nat, codes, scales, c, copies):
-            for h in range(CHUNK_TILES // 2):
-                t = c * CHUNK_TILES + 2 * h
-                cols = slice(t * P, (t + 2) * P)
-                quantise_two_tiles(nat[:, t : t + 2, :], codes[:, cols], scales[:, cols], copies[h % len(copies)])
+        hid_n = {}
+        acc_r = {}
+        acc_z = {}
+        acc_n = {}
+        hw_acc = {}
+        hw = {}
+        reset = {}
+        fresh = {}
+        pre = {}
+        cand = {}
+        part = {}
+        sums = {}
 
-        def quantise_weights(f, copies):
-            for h in range(3):
-                quantise_two_tiles(
-                    w_nat[:, f, 2 * h : 2 * h + 2, :],
-                    w_codes[:, f, 2 * h : 2 * h + 2, :].rearrange("p i m -> p (i m)"),
-                    w_scales[:, f, 2 * h : 2 * h + 2, :].rearrange("p i m -> p (i m)"),
-                    copies[h % len(copies)],
+        def weight_pass(acc, f, g, moving, start, stop):
+            nc.tensor.matmul_mx(
+                out=acc[:],
+                lhsT=w_codes[:, f, g, :].bitcast(FP8X4),
+                lhsT_scale=w_scales[:, f, g, :],
+                rhs=moving[0].bitcast(FP8X4),
+                rhs_scale=moving[1],
+                start=start,
+                stop=stop,
+            )
+
+        def products(s):
+            b, d = divmod(s, DIRS)
+            c, f = divmod(b, FEAT_TILES)
+            nodes = slice(c * CHUNK, (c + 1) * CHUNK)
+            xq = (x_codes[:, nodes], x_scales[:, nodes])
+            aq = (agg_codes[:, d, nodes], agg_scales[:, d, nodes])
+            if d == 0:
+                h_n = psum.tile([P, CHUNK], F32, tag="hn", bufs=1)
+                weight_pass(h_n, f, HH_N, xq, True, True)
+                hid_n[b] = h_n
+            a_r = psum.tile([P, CHUNK], F32, tag="gate", bufs=4)
+            weight_pass(a_r, f, IH_R, aq, True, False)
+            weight_pass(a_r, f, HH_R, xq, False, True)
+            a_z = psum.tile([P, CHUNK], F32, tag="gate", bufs=4)
+            weight_pass(a_z, f, IH_Z, aq, True, False)
+            weight_pass(a_z, f, HH_Z, xq, False, True)
+            a_n = psum.tile([P, CHUNK], F32, tag="gate", bufs=4)
+            weight_pass(a_n, f, IH_N, aq, True, True)
+            acc_r[s] = a_r
+            acc_z[s] = a_z
+            acc_n[s] = a_n
+            if d == DIRS - 1:
+                feats = slice(f * P, (f + 1) * P)
+                a_hw = psum.tile([P, CHUNK], F32, tag="gate", bufs=4)
+                nc.tensor.matmul_mx(
+                    out=a_hw[:], lhsT=wh_codes[:, feats].bitcast(FP8X4), lhsT_scale=wh_scales[:, feats],
+                    rhs=xq[0].bitcast(FP8X4), rhs_scale=xq[1], start=True, stop=True,
                 )
+                hw_acc[b] = a_hw
 
-        both = [nc.scalar.copy, nc.vector.tensor_copy]
-        scalar_only = [nc.scalar.copy]
+        def gates(s):
+            b, d = divmod(s, DIRS)
+            f = b % FEAT_TILES
+            r = work.tile([P, CHUNK], F32, tag="reset")
+            nc.scalar.activation(out=r[:], in_=acc_r[s][:], func=ACT.Sigmoid, bias=b_r[:, f : f + 1])
+            fr = work.tile([P, CHUNK], F32, tag="fresh", bufs=7)
+            nc.scalar.activation(
+                out=fr[:], in_=acc_z[s][:], func=ACT.Sigmoid, bias=minus_b_z[:, f : f + 1], scale=-1.0
+            )
+            reset[s] = r
+            fresh[s] = fr
+            if d == DIRS - 1:
+                t = work.tile([P, CHUNK], F32, tag="hw")
+                nc.scalar.activation(out=t[:], in_=hw_acc[b][:], func=ACT.Relu, bias=bias_cols[:, BH + f : BH + f + 1])
+                hw[b] = t
+
+        def candidate_input(s):
+            b = s // DIRS
+            f = b % FEAT_TILES
+            a = work.tile([P, CHUNK], F32, tag="pre")
+            nc.vector.scalar_tensor_tensor(
+                out=a[:], in0=hid_n[b][:], scalar=bias_cols[:, BHH_N + f : BHH_N + f + 1], in1=reset[s][:],
+                op0=ALU.add, op1=ALU.mult,
+            )
+            nc.vector.tensor_tensor(out=a[:], in0=acc_n[s][:], in1=a[:], op=ALU.add)
+            pre[s] = a
+
+        def candidate(s):
+            f = (s // DIRS) % FEAT_TILES
+            cd = work.tile([P, CHUNK], F32, tag="cand")
+            nc.scalar.activation(out=cd[:], in_=pre[s][:], func=ACT.Tanh, bias=bias_cols[:, BIH_N + f : BIH_N + f + 1])
+            cand[s] = cd
+
+        def blend(s):
+            pt = work.tile([P, CHUNK], F32, tag="part", bufs=7)
+            nc.vector.tensor_tensor(out=pt[:], in0=fresh[s][:], in1=cand[s][:], op=ALU.mult)
+            part[s] = pt
+
+        def back_to_nodes(b):
+            steps = range(b * DIRS, (b + 1) * DIRS)
+            fresh_sum = psum.tile([P, CHUNK], F32, tag="node", bufs=3)
+            part_sum = psum.tile([P, CHUNK], F32, tag="node", bufs=3)
+            hw_nodes = psum.tile([P, CHUNK], F32, tag="node", bufs=3)
+            for total, terms in (
+                (fresh_sum, [fresh[s] for s in steps]),
+                (part_sum, [part[s] for s in steps]),
+                (hw_nodes, [hw[b]]),
+            ):
+                for j in range(CHUNK_TILES):
+                    cols = slice(j * P, (j + 1) * P)
+                    for i, term in enumerate(terms):
+                        nc.tensor.matmul(
+                            out=total[:, cols], lhsT=term[:, cols], rhs=ident[:], is_transpose=True,
+                            start=(i == 0), stop=(i == len(terms) - 1),
+                        )
+            sums[b] = (fresh_sum, part_sum, hw_nodes)
+
+        def by_tile(t):
+            return t[:].rearrange("p (j m) -> p j m", j=CHUNK_TILES)
+
+        def finish(b):
+            c, f = divmod(b, FEAT_TILES)
+            feats = slice(f * P, (f + 1) * P)
+            fresh_sum, part_sum, hw_nodes = sums[b]
+            x_blk = x_nat[:, chunk_tiles(c), feats]
+            minus_zh = work.tile([P, CHUNK], F32, tag="minus_zh")
+            nc.vector.scalar_tensor_tensor(
+                out=by_tile(minus_zh), in0=by_tile(fresh_sum), scalar=float(DIRS), in1=x_blk,
+                op0=ALU.subtract, op1=ALU.mult,
+            )
+            hsum = work.tile([P, CHUNK], F32, tag="hsum")
+            nc.vector.tensor_tensor(out=hsum[:], in0=part_sum[:], in1=minus_zh[:], op=ALU.subtract)
+            diff = work.tile([P, CHUNK], F32, tag="diff")
+            nc.vector.scalar_tensor_tensor(
+                out=by_tile(diff), in0=by_tile(hsum), scalar=0.0, in1=x_blk, op0=ALU.max, op1=ALU.subtract
+            )
+            gated = work.tile([P, CHUNK], F32, tag="gated")
+            nc.vector.tensor_tensor(out=gated[:], in0=hw_nodes[:], in1=diff[:], op=ALU.mult)
+            result = work.tile([P, CHUNK], F32, tag="result", bufs=3)
+            nc.vector.tensor_tensor(out=by_tile(result), in0=by_tile(gated), in1=x_blk, op=ALU.add)
+            nc.sync.dma_start(out=out_view[:, chunk_tiles(c), feats], in_=by_tile(result))
+
+        first = node_units(x_nat, x_codes, x_scales, 0)
+        first.extend(node_units(agg_nat[:, 0], agg_codes[:, 0], agg_scales[:, 0], 0))
+        first.extend(weight_units(0))
+        for i, unit in enumerate(first):
+            quantise(unit, regroup(flip(unit), nc.vector.tensor_copy if i % 2 else nc.scalar.copy))
 
         bias_rows32 = keep.tile([P, P], F32)
         nc.vector.tensor_copy(out=bias_rows32[:], in_=bias_rows[:])
@@ -132,121 +291,48 @@ def tile_graphconvolution_pb_kernel(tc, agg, x, wih, whh, bih, bhh, wh, bh, out)
         bias_cols = keep.tile([P, 32], F32)
         nc.vector.tensor_copy(out=bias_cols[:], in_=bias_flipped[:, 0:32])
         b_r = keep.tile([P, FEAT_TILES], F32)
-        nc.vector.tensor_tensor(out=b_r[:], in0=bias_cols[:, 0:4], in1=bias_cols[:, 12:16], op=ALU.add)
+        nc.vector.tensor_tensor(
+            out=b_r[:], in0=bias_cols[:, BIH_R : BIH_R + FEAT_TILES], in1=bias_cols[:, BHH_R : BHH_R + FEAT_TILES],
+            op=ALU.add,
+        )
         minus_b_z = keep.tile([P, FEAT_TILES], F32)
         nc.vector.scalar_tensor_tensor(
-            out=minus_b_z[:], in0=bias_cols[:, 4:8], scalar=-1.0, in1=bias_cols[:, 16:20],
-            op0=ALU.mult, op1=ALU.subtract,
+            out=minus_b_z[:], in0=bias_cols[:, BIH_Z : BIH_Z + FEAT_TILES], scalar=-1.0,
+            in1=bias_cols[:, BHH_Z : BHH_Z + FEAT_TILES], op0=ALU.mult, op1=ALU.subtract,
         )
 
-        quantise_nodes(x_nat, x_codes, x_scales, 0, both)
-        quantise_weights(0, both)
-        quantise_nodes(agg_nat[:, 0], agg_codes[:, 0], agg_scales[:, 0], 0, both)
-        wh_grouped = stage.tile([P, FEATS, PACK], BF16, align_bytes=64, bufs=1)
-        nc.vector.tensor_copy(out=wh_grouped[:], in_=wh_nat[:].rearrange("p t o -> p o t"))
-        nc.vector.quantize_mx(
-            out=wh_codes[:].bitcast(FP8X4), scales=wh_scales[:], in_=wh_grouped[:].rearrange("p o t -> p (o t)")
-        )
+        jobs = [node_units(agg_nat[:, d], agg_codes[:, d], agg_scales[:, d], 0) for d in range(1, DIRS)]
+        jobs.extend([weight_units(f) for f in range(1, FEAT_TILES)])
+        jobs.append(node_units(x_nat, x_codes, x_scales, 1))
+        jobs.extend([node_units(agg_nat[:, d], agg_codes[:, d], agg_scales[:, d], 1) for d in range(DIRS)])
 
-        def weight_pass(acc, f, g, codes, scales, start, stop):
-            nc.tensor.matmul_mx(
-                out=acc[:],
-                lhsT=w_codes[:, f, g, :].bitcast(FP8X4),
-                lhsT_scale=w_scales[:, f, g, :],
-                rhs=codes.bitcast(FP8X4),
-                rhs_scale=scales,
-                start=start,
-                stop=stop,
-            )
-
-        def by_tile(t):
-            return t[:].rearrange("p (j m) -> p j m", j=CHUNK_TILES)
-
-        for c in range(CHUNKS):
-            nodes = slice(c * CHUNK, (c + 1) * CHUNK)
-            xq = (x_codes[:, nodes], x_scales[:, nodes])
-            for f in range(FEAT_TILES):
-                feats = slice(f * P, (f + 1) * P)
-                if c == 0:
-                    if f + 1 < FEAT_TILES:
-                        quantise_weights(f + 1, scalar_only)
-                    if f == 0:
-                        quantise_nodes(x_nat, x_codes, x_scales, 1, scalar_only)
-                    else:
-                        quantise_nodes(agg_nat[:, f - 1], agg_codes[:, f - 1], agg_scales[:, f - 1], 1, scalar_only)
-
-                hid_n = psum.tile([P, CHUNK], F32, tag="hn", bufs=1)
-                weight_pass(hid_n, f, HH_N, xq[0], xq[1], True, True)
-                hw_acc = psum.tile([P, CHUNK], F32, tag="gate", bufs=4)
-                nc.tensor.matmul_mx(
-                    out=hw_acc[:], lhsT=wh_codes[:, feats].bitcast(FP8X4), lhsT_scale=wh_scales[:, feats],
-                    rhs=xq[0].bitcast(FP8X4), rhs_scale=xq[1], start=True, stop=True,
-                )
-                hw = work.tile([P, CHUNK], F32, tag="hw")
-                nc.scalar.activation(out=hw[:], in_=hw_acc[:], func=ACT.Relu, bias=bias_cols[:, 24 + f : 25 + f])
-
-                fresh = []
-                part = []
-                for d in range(DIRS):
-                    if c == 0 and f == 0 and d + 1 < DIRS:
-                        quantise_nodes(agg_nat[:, d + 1], agg_codes[:, d + 1], agg_scales[:, d + 1], 0, scalar_only)
-                    aq = (agg_codes[:, d, nodes], agg_scales[:, d, nodes])
-                    acc_r = psum.tile([P, CHUNK], F32, tag="gate", bufs=4)
-                    weight_pass(acc_r, f, IH_R, aq[0], aq[1], True, False)
-                    weight_pass(acc_r, f, HH_R, xq[0], xq[1], False, True)
-                    acc_z = psum.tile([P, CHUNK], F32, tag="gate", bufs=4)
-                    weight_pass(acc_z, f, IH_Z, aq[0], aq[1], True, False)
-                    weight_pass(acc_z, f, HH_Z, xq[0], xq[1], False, True)
-                    acc_n = psum.tile([P, CHUNK], F32, tag="gate", bufs=4)
-                    weight_pass(acc_n, f, IH_N, aq[0], aq[1], True, True)
-
-                    reset = work.tile([P, CHUNK], F32, tag="reset")
-                    nc.scalar.activation(out=reset[:], in_=acc_r[:], func=ACT.Sigmoid, bias=b_r[:, f : f + 1])
-                    fresh_d = work.tile([P, CHUNK], F32, tag="fresh", bufs=6)
-                    nc.scalar.activation(
-                        out=fresh_d[:], in_=acc_z[:], func=ACT.Sigmoid, bias=minus_b_z[:, f : f + 1], scale=-1.0
-                    )
-                    pre = work.tile([P, CHUNK], F32, tag="pre")
-                    nc.vector.scalar_tensor_tensor(
-                        out=pre[:], in0=hid_n[:], scalar=bias_cols[:, 20 + f : 21 + f], in1=reset[:],
-                        op0=ALU.add, op1=ALU.mult,
-                    )
-                    nc.vector.tensor_tensor(out=pre[:], in0=acc_n[:], in1=pre[:], op=ALU.add)
-                    cand = work.tile([P, CHUNK], F32, tag="cand")
-                    nc.scalar.activation(out=cand[:], in_=pre[:], func=ACT.Tanh, bias=bias_cols[:, 8 + f : 9 + f])
-                    part_d = work.tile([P, CHUNK], F32, tag="part", bufs=6)
-                    nc.vector.tensor_tensor(out=part_d[:], in0=fresh_d[:], in1=cand[:], op=ALU.mult)
-                    fresh.append(fresh_d)
-                    part.append(part_d)
-
-                fresh_sum = psum.tile([P, CHUNK], F32, tag="node", bufs=3)
-                part_sum = psum.tile([P, CHUNK], F32, tag="node", bufs=3)
-                hw_nodes = psum.tile([P, CHUNK], F32, tag="node", bufs=3)
-                for total, terms in ((fresh_sum, fresh), (part_sum, part), (hw_nodes, [hw])):
-                    for j in range(CHUNK_TILES):
-                        cols = slice(j * P, (j + 1) * P)
-                        for i, term in enumerate(terms):
-                            nc.tensor.matmul(
-                                out=total[:, cols], lhsT=term[:, cols], rhs=ident[:], is_transpose=True,
-                                start=(i == 0), stop=(i == len(terms) - 1),
-                            )
-
-                x_blk = x_nat[:, c * CHUNK_TILES : (c + 1) * CHUNK_TILES, feats]
-                minus_zh = work.tile([P, CHUNK], F32, tag="minus_zh")
-                nc.vector.scalar_tensor_tensor(
-                    out=by_tile(minus_zh), in0=by_tile(fresh_sum), scalar=float(DIRS), in1=x_blk,
-                    op0=ALU.subtract, op1=ALU.mult,
-                )
-                hsum = work.tile([P, CHUNK], F32, tag="hsum")
-                nc.vector.tensor_tensor(out=hsum[:], in0=part_sum[:], in1=minus_zh[:], op=ALU.subtract)
-                diff = work.tile([P, CHUNK], F32, tag="diff")
-                nc.vector.scalar_tensor_tensor(
-                    out=by_tile(diff), in0=by_tile(hsum), scalar=0.0, in1=x_blk, op0=ALU.max, op1=ALU.subtract
-                )
-                gated = work.tile([P, CHUNK], F32, tag="gated")
-                nc.vector.tensor_tensor(out=gated[:], in0=hw_nodes[:], in1=diff[:], op=ALU.mult)
-                result = work.tile([P, CHUNK], F32, tag="result", bufs=3)
-                nc.vector.tensor_tensor(out=by_tile(result), in0=by_tile(gated), in1=x_blk, op=ALU.add)
-                nc.sync.dma_start(
-                    out=out_view[:, c * CHUNK_TILES : (c + 1) * CHUNK_TILES, feats], in_=by_tile(result)
+        copied = []
+        for i in range(-2, STEPS + 3):
+            if 0 <= i + 1 < STEPS:
+                products(i + 1)
+            job = jobs[i + 2] if i + 2 < len(jobs) else []
+            flipped = [flip(unit) for unit in job]
+            if 0 <= i < STEPS:
+                candidate_input(i)
+            if 0 <= i + 1 < STEPS:
+                gates(i + 1)
+            if 0 <= i < STEPS:
+                candidate(i)
+            copying = [(unit, regroup(fl, nc.scalar.copy)) for unit, fl in zip(job, flipped)]
+            if i == 0:
+                wh_grouped = keep.tile([P, FEATS, PACK], BF16, align_bytes=64)
+                nc.vector.tensor_copy(out=wh_grouped[:], in_=wh_nat[:].rearrange("p t o -> p o t"))
+            if 0 <= i - 1 < STEPS:
+                blend(i - 1)
+            if 0 <= i - 2 < STEPS and (i - 2) % DIRS == DIRS - 1:
+                back_to_nodes((i - 2) // DIRS)
+            if 0 <= i - 3 < STEPS and (i - 3) % DIRS == DIRS - 1:
+                finish((i - 3) // DIRS)
+            for unit, grouped in copied:
+                quantise(unit, grouped)
+            copied = copying
+            if i == 0:
+                nc.vector.quantize_mx(
+                    out=wh_codes[:].bitcast(FP8X4), scales=wh_scales[:],
+                    in_=wh_grouped[:].rearrange("p o t -> p (o t)"),
                 )

@@ -75,9 +75,12 @@ def tile_graphconvolution_pb_kernel(tc, agg, x, wih, whh, bih, bhh, wh, bh, out)
             nc.sync.dma_start(out=w_nat[:, f, IH_R : IH_N + 1, :], in_=wih_view[f])
 
         nc.vector.memset(bias_rows[:], 0.0)
+        warm = keep.tile([P, 1], F32)
+        nc.vector.memset(warm[:], 0.0)
         nc.scalar.dma_start(out=bias_rows[BIH_R:BHH_R, :], in_=bih.rearrange("(r m) -> r m", m=P))
         nc.scalar.dma_start(out=bias_rows[BHH_R:BH, :], in_=bhh.rearrange("(r m) -> r m", m=P))
         nc.scalar.dma_start(out=bias_rows[BH : BH + FEAT_TILES, :], in_=bh.rearrange("(r m) -> r m", m=P))
+        nc.scalar.activation(out=warm[:], in_=warm[:], func=ACT.Sigmoid)
         load_x(0)
         load_agg(0, 0)
         load_weights(0)
@@ -153,7 +156,13 @@ def tile_graphconvolution_pb_kernel(tc, agg, x, wih, whh, bih, bhh, wh, bh, out)
         pre = {}
         cand = {}
         part = {}
-        sums = {}
+        fresh_sum = {}
+        part_sum = {}
+        hw_nodes = {}
+        minus_zh = {}
+        hsum = {}
+        diff = {}
+        gated = {}
 
         def weight_pass(acc, f, g, moving, start, stop):
             nc.tensor.matmul_mx(
@@ -172,13 +181,13 @@ def tile_graphconvolution_pb_kernel(tc, agg, x, wih, whh, bih, bhh, wh, bh, out)
             nodes = slice(c * CHUNK, (c + 1) * CHUNK)
             xq = (x_codes[:, nodes], x_scales[:, nodes])
             aq = (agg_codes[:, d, nodes], agg_scales[:, d, nodes])
+            a_r = psum.tile([P, CHUNK], F32, tag="gate", bufs=4)
+            weight_pass(a_r, f, IH_R, aq, True, False)
+            weight_pass(a_r, f, HH_R, xq, False, True)
             if d == 0:
                 h_n = psum.tile([P, CHUNK], F32, tag="hn", bufs=1)
                 weight_pass(h_n, f, HH_N, xq, True, True)
                 hid_n[b] = h_n
-            a_r = psum.tile([P, CHUNK], F32, tag="gate", bufs=4)
-            weight_pass(a_r, f, IH_R, aq, True, False)
-            weight_pass(a_r, f, HH_R, xq, False, True)
             a_z = psum.tile([P, CHUNK], F32, tag="gate", bufs=4)
             weight_pass(a_z, f, IH_Z, aq, True, False)
             weight_pass(a_z, f, HH_Z, xq, False, True)
@@ -212,7 +221,7 @@ def tile_graphconvolution_pb_kernel(tc, agg, x, wih, whh, bih, bhh, wh, bh, out)
                 nc.scalar.activation(out=t[:], in_=hw_acc[b][:], func=ACT.Relu, bias=bias_cols[:, BH + f : BH + f + 1])
                 hw[b] = t
 
-        def candidate_input(s):
+        def reset_hidden(s):
             b = s // DIRS
             f = b % FEAT_TILES
             a = work.tile([P, CHUNK], F32, tag="pre")
@@ -220,8 +229,10 @@ def tile_graphconvolution_pb_kernel(tc, agg, x, wih, whh, bih, bhh, wh, bh, out)
                 out=a[:], in0=hid_n[b][:], scalar=bias_cols[:, BHH_N + f : BHH_N + f + 1], in1=reset[s][:],
                 op0=ALU.add, op1=ALU.mult,
             )
-            nc.vector.tensor_tensor(out=a[:], in0=acc_n[s][:], in1=a[:], op=ALU.add)
             pre[s] = a
+
+        def candidate_input(s):
+            nc.vector.tensor_tensor(out=pre[s][:], in0=acc_n[s][:], in1=pre[s][:], op=ALU.add)
 
         def candidate(s):
             f = (s // DIRS) % FEAT_TILES
@@ -234,100 +245,149 @@ def tile_graphconvolution_pb_kernel(tc, agg, x, wih, whh, bih, bhh, wh, bh, out)
             nc.vector.tensor_tensor(out=pt[:], in0=fresh[s][:], in1=cand[s][:], op=ALU.mult)
             part[s] = pt
 
-        def back_to_nodes(b):
-            steps = range(b * DIRS, (b + 1) * DIRS)
-            fresh_sum = psum.tile([P, CHUNK], F32, tag="node", bufs=3)
-            part_sum = psum.tile([P, CHUNK], F32, tag="node", bufs=3)
-            hw_nodes = psum.tile([P, CHUNK], F32, tag="node", bufs=3)
-            for total, terms in (
-                (fresh_sum, [fresh[s] for s in steps]),
-                (part_sum, [part[s] for s in steps]),
-                (hw_nodes, [hw[b]]),
-            ):
-                for j in range(CHUNK_TILES):
-                    cols = slice(j * P, (j + 1) * P)
-                    for i, term in enumerate(terms):
-                        nc.tensor.matmul(
-                            out=total[:, cols], lhsT=term[:, cols], rhs=ident[:], is_transpose=True,
-                            start=(i == 0), stop=(i == len(terms) - 1),
-                        )
-            sums[b] = (fresh_sum, part_sum, hw_nodes)
+        def back_to_nodes(terms):
+            total = psum.tile([P, CHUNK], F32, tag="node", bufs=3)
+            for j in range(CHUNK_TILES):
+                cols = slice(j * P, (j + 1) * P)
+                for i, term in enumerate(terms):
+                    nc.tensor.matmul(
+                        out=total[:, cols], lhsT=term[:, cols], rhs=ident[:], is_transpose=True,
+                        start=(i == 0), stop=(i == len(terms) - 1),
+                    )
+            return total
 
         def by_tile(t):
             return t[:].rearrange("p (j m) -> p j m", j=CHUNK_TILES)
 
-        def finish(b):
+        def place(b):
             c, f = divmod(b, FEAT_TILES)
-            feats = slice(f * P, (f + 1) * P)
-            fresh_sum, part_sum, hw_nodes = sums[b]
-            x_blk = x_nat[:, chunk_tiles(c), feats]
-            minus_zh = work.tile([P, CHUNK], F32, tag="minus_zh")
+            return chunk_tiles(c), slice(f * P, (f + 1) * P)
+
+        def x_of(b):
+            tiles, feats = place(b)
+            return x_nat[:, tiles, feats]
+
+        def finish_zh(b):
+            t = work.tile([P, CHUNK], F32, tag="minus_zh")
             nc.vector.scalar_tensor_tensor(
-                out=by_tile(minus_zh), in0=by_tile(fresh_sum), scalar=float(DIRS), in1=x_blk,
+                out=by_tile(t), in0=by_tile(fresh_sum[b]), scalar=float(DIRS), in1=x_of(b),
                 op0=ALU.subtract, op1=ALU.mult,
             )
-            hsum = work.tile([P, CHUNK], F32, tag="hsum")
-            nc.vector.tensor_tensor(out=hsum[:], in0=part_sum[:], in1=minus_zh[:], op=ALU.subtract)
-            diff = work.tile([P, CHUNK], F32, tag="diff")
+            minus_zh[b] = t
+
+        def finish_sum(b):
+            t = work.tile([P, CHUNK], F32, tag="hsum")
+            nc.vector.tensor_tensor(out=t[:], in0=part_sum[b][:], in1=minus_zh[b][:], op=ALU.subtract)
+            hsum[b] = t
+
+        def finish_diff(b):
+            t = work.tile([P, CHUNK], F32, tag="diff")
             nc.vector.scalar_tensor_tensor(
-                out=by_tile(diff), in0=by_tile(hsum), scalar=0.0, in1=x_blk, op0=ALU.max, op1=ALU.subtract
+                out=by_tile(t), in0=by_tile(hsum[b]), scalar=0.0, in1=x_of(b), op0=ALU.max, op1=ALU.subtract
             )
-            gated = work.tile([P, CHUNK], F32, tag="gated")
-            nc.vector.tensor_tensor(out=gated[:], in0=hw_nodes[:], in1=diff[:], op=ALU.mult)
+            diff[b] = t
+
+        def finish_gate(b):
+            t = work.tile([P, CHUNK], F32, tag="gated")
+            nc.vector.tensor_tensor(out=t[:], in0=hw_nodes[b][:], in1=diff[b][:], op=ALU.mult)
+            gated[b] = t
+
+        def finish_out(b):
+            tiles, feats = place(b)
             result = work.tile([P, CHUNK], F32, tag="result", bufs=3)
-            nc.vector.tensor_tensor(out=by_tile(result), in0=by_tile(gated), in1=x_blk, op=ALU.add)
-            nc.sync.dma_start(out=out_view[:, chunk_tiles(c), feats], in_=by_tile(result))
+            nc.vector.tensor_tensor(out=by_tile(result), in0=by_tile(gated[b]), in1=x_of(b), op=ALU.add)
+            nc.sync.dma_start(out=out_view[:, tiles, feats], in_=by_tile(result))
+
+        bias_rows32 = keep.tile([P, P], F32)
+        nc.vector.tensor_copy(out=bias_rows32[:], in_=bias_rows[:])
+
+        def bias_columns():
+            bias_flipped = psum.tile([P, P], F32, tag="node", bufs=3)
+            nc.tensor.transpose(bias_flipped[:], bias_rows32[:], ident[:])
+            nc.vector.tensor_copy(out=bias_cols[:], in_=bias_flipped[:, 0:32])
+            nc.vector.tensor_tensor(
+                out=b_r[:], in0=bias_cols[:, BIH_R : BIH_R + FEAT_TILES],
+                in1=bias_cols[:, BHH_R : BHH_R + FEAT_TILES], op=ALU.add,
+            )
+            nc.vector.scalar_tensor_tensor(
+                out=minus_b_z[:], in0=bias_cols[:, BIH_Z : BIH_Z + FEAT_TILES], scalar=-1.0,
+                in1=bias_cols[:, BHH_Z : BHH_Z + FEAT_TILES], op0=ALU.mult, op1=ALU.subtract,
+            )
+
+        bias_cols = keep.tile([P, 32], F32)
+        b_r = keep.tile([P, FEAT_TILES], F32)
+        minus_b_z = keep.tile([P, FEAT_TILES], F32)
 
         first = node_units(x_nat, x_codes, x_scales, 0)
         first.extend(node_units(agg_nat[:, 0], agg_codes[:, 0], agg_scales[:, 0], 0))
         first.extend(weight_units(0))
+        waiting = []
         for i, unit in enumerate(first):
-            quantise(unit, regroup(flip(unit), nc.vector.tensor_copy if i % 2 else nc.scalar.copy))
+            waiting.append((unit, regroup(flip(unit), nc.vector.tensor_copy if i % 2 else nc.scalar.copy)))
+            if i == 3:
+                bias_columns()
+            if len(waiting) > 1:
+                quantise(*waiting.pop(0))
+        quantise(*waiting.pop(0))
 
-        bias_rows32 = keep.tile([P, P], F32)
-        nc.vector.tensor_copy(out=bias_rows32[:], in_=bias_rows[:])
-        bias_flipped = psum.tile([P, P], F32, tag="node", bufs=3)
-        nc.tensor.transpose(bias_flipped[:], bias_rows32[:], ident[:])
-        bias_cols = keep.tile([P, 32], F32)
-        nc.vector.tensor_copy(out=bias_cols[:], in_=bias_flipped[:, 0:32])
-        b_r = keep.tile([P, FEAT_TILES], F32)
-        nc.vector.tensor_tensor(
-            out=b_r[:], in0=bias_cols[:, BIH_R : BIH_R + FEAT_TILES], in1=bias_cols[:, BHH_R : BHH_R + FEAT_TILES],
-            op=ALU.add,
-        )
-        minus_b_z = keep.tile([P, FEAT_TILES], F32)
-        nc.vector.scalar_tensor_tensor(
-            out=minus_b_z[:], in0=bias_cols[:, BIH_Z : BIH_Z + FEAT_TILES], scalar=-1.0,
-            in1=bias_cols[:, BHH_Z : BHH_Z + FEAT_TILES], op0=ALU.mult, op1=ALU.subtract,
-        )
+        units = []
+        for d in range(1, DIRS):
+            units.extend(node_units(agg_nat[:, d], agg_codes[:, d], agg_scales[:, d], 0))
+        for f in range(1, FEAT_TILES):
+            units.extend(weight_units(f))
+        units.extend(node_units(x_nat, x_codes, x_scales, 1))
+        for d in range(DIRS):
+            units.extend(node_units(agg_nat[:, d], agg_codes[:, d], agg_scales[:, d], 1))
 
-        jobs = [node_units(agg_nat[:, d], agg_codes[:, d], agg_scales[:, d], 0) for d in range(1, DIRS)]
-        jobs.extend([weight_units(f) for f in range(1, FEAT_TILES)])
-        jobs.append(node_units(x_nat, x_codes, x_scales, 1))
-        jobs.extend([node_units(agg_nat[:, d], agg_codes[:, d], agg_scales[:, d], 1) for d in range(DIRS)])
+        def share(i):
+            if i <= 0:
+                return 3 if i == 0 else 2
+            return 2 if i % DIRS == 2 else 1
+
+        def ending(j):
+            return j // DIRS if 0 <= j < STEPS and j % DIRS == DIRS - 1 else None
 
         copied = []
-        for i in range(-2, STEPS + 3):
+        for i in range(-2, STEPS + 4):
             if 0 <= i + 1 < STEPS:
                 products(i + 1)
-            job = jobs[i + 2] if i + 2 < len(jobs) else []
+            job = [units.pop(0) for n in range(min(share(i), len(units)))]
             flipped = [flip(unit) for unit in job]
             if 0 <= i < STEPS:
-                candidate_input(i)
+                reset_hidden(i)
             if 0 <= i + 1 < STEPS:
                 gates(i + 1)
+            for b in [ending(i - 2)]:
+                if b is not None:
+                    finish_zh(b)
+            for b in [ending(i - 3)]:
+                if b is not None:
+                    finish_sum(b)
+            for b in [ending(i - 4)]:
+                if b is not None:
+                    finish_gate(b)
             if 0 <= i < STEPS:
+                candidate_input(i)
                 candidate(i)
             copying = [(unit, regroup(fl, nc.scalar.copy)) for unit, fl in zip(job, flipped)]
             if i == 0:
                 wh_grouped = keep.tile([P, FEATS, PACK], BF16, align_bytes=64)
                 nc.vector.tensor_copy(out=wh_grouped[:], in_=wh_nat[:].rearrange("p t o -> p o t"))
+            for b in [ending(i - 3)]:
+                if b is not None:
+                    finish_diff(b)
+                    hw_nodes[b] = back_to_nodes([hw[b]])
             if 0 <= i - 1 < STEPS:
                 blend(i - 1)
-            if 0 <= i - 2 < STEPS and (i - 2) % DIRS == DIRS - 1:
-                back_to_nodes((i - 2) // DIRS)
-            if 0 <= i - 3 < STEPS and (i - 3) % DIRS == DIRS - 1:
-                finish((i - 3) // DIRS)
+            for b in [ending(i - 4)]:
+                if b is not None:
+                    finish_out(b)
+            for b in [ending(i - 1)]:
+                if b is not None:
+                    fresh_sum[b] = back_to_nodes([fresh[b * DIRS + d] for d in range(DIRS)])
+            for b in [ending(i - 2)]:
+                if b is not None:
+                    part_sum[b] = back_to_nodes([part[b * DIRS + d] for d in range(DIRS)])
             for unit, grouped in copied:
                 quantise(unit, grouped)
             copied = copying

@@ -242,7 +242,7 @@ def tile_graphconvolution_pb_kernel(tc, agg, x, wih, whh, bih, bhh, wh, bh, out)
 
         def blend(s):
             pt = work.tile([P, CHUNK], F32, tag="part", bufs=7)
-            nc.vector.tensor_tensor(out=pt[:], in0=fresh[s][:], in1=cand[s][:], op=ALU.mult)
+            nc.gpsimd.tensor_tensor(out=pt[:], in0=fresh[s][:], in1=cand[s][:], op=ALU.mult)
             part[s] = pt
 
         def back_to_nodes(terms):
@@ -369,6 +369,7 @@ def tile_graphconvolution_pb_kernel(tc, agg, x, wih, whh, bih, bhh, wh, bh, out)
             if 0 <= i < STEPS:
                 candidate_input(i)
                 candidate(i)
+                blend(i)
             copying = [(unit, regroup(fl, nc.scalar.copy)) for unit, fl in zip(job, flipped)]
             if i == 0:
                 wh_grouped = keep.tile([P, FEATS, PACK], BF16, align_bytes=64)
@@ -377,8 +378,6 @@ def tile_graphconvolution_pb_kernel(tc, agg, x, wih, whh, bih, bhh, wh, bh, out)
                 if b is not None:
                     finish_diff(b)
                     hw_nodes[b] = back_to_nodes([hw[b]])
-            if 0 <= i - 1 < STEPS:
-                blend(i - 1)
             for b in [ending(i - 4)]:
                 if b is not None:
                     finish_out(b)

@@ -77,11 +77,11 @@ def tile_graphconvolution_pb_kernel(tc, agg, x, wih, whh, bih, bhh, wh, bh, out)
         nc.vector.memset(bias_rows[:], 0.0)
         warm = keep.tile([P, 1], F32)
         nc.vector.memset(warm[:], 0.0)
-        nc.scalar.dma_start(out=bias_rows[BIH_R:BHH_R, :], in_=bih.rearrange("(r m) -> r m", m=P))
-        nc.scalar.dma_start(out=bias_rows[BHH_R:BH, :], in_=bhh.rearrange("(r m) -> r m", m=P))
-        nc.scalar.dma_start(out=bias_rows[BH : BH + FEAT_TILES, :], in_=bh.rearrange("(r m) -> r m", m=P))
         nc.scalar.activation(out=warm[:], in_=warm[:], func=ACT.Sigmoid)
         load_x(0)
+        nc.sync.dma_start(out=bias_rows[BIH_R:BHH_R, :], in_=bih.rearrange("(r m) -> r m", m=P))
+        nc.sync.dma_start(out=bias_rows[BHH_R:BH, :], in_=bhh.rearrange("(r m) -> r m", m=P))
+        nc.sync.dma_start(out=bias_rows[BH : BH + FEAT_TILES, :], in_=bh.rearrange("(r m) -> r m", m=P))
         load_agg(0, 0)
         load_weights(0)
         load_agg(1, 0)
@@ -161,7 +161,8 @@ def tile_graphconvolution_pb_kernel(tc, agg, x, wih, whh, bih, bhh, wh, bh, out)
         hw_nodes = {}
         minus_zh = {}
         hsum = {}
-        diff = {}
+        minus_skip = {}
+        fresh_total = {}
         gated = {}
 
         def weight_pass(acc, f, g, moving, start, stop):
@@ -245,6 +246,12 @@ def tile_graphconvolution_pb_kernel(tc, agg, x, wih, whh, bih, bhh, wh, bh, out)
             nc.gpsimd.tensor_tensor(out=pt[:], in0=fresh[s][:], in1=cand[s][:], op=ALU.mult)
             part[s] = pt
 
+        def add_fresh(s):
+            t = work.tile([P, CHUNK], F32, tag="fresh_total", bufs=3)
+            before = fresh[s - 1] if s % DIRS == 1 else fresh_total[s - 1]
+            nc.gpsimd.tensor_tensor(out=t[:], in0=before[:], in1=fresh[s][:], op=ALU.add)
+            fresh_total[s] = t
+
         def back_to_nodes(terms):
             total = psum.tile([P, CHUNK], F32, tag="node", bufs=3)
             for j in range(CHUNK_TILES):
@@ -280,26 +287,27 @@ def tile_graphconvolution_pb_kernel(tc, agg, x, wih, whh, bih, bhh, wh, bh, out)
             nc.vector.tensor_tensor(out=t[:], in0=part_sum[b][:], in1=minus_zh[b][:], op=ALU.subtract)
             hsum[b] = t
 
-        def finish_diff(b):
-            t = work.tile([P, CHUNK], F32, tag="diff")
+        def finish_skip(b):
+            t = work.tile([P, CHUNK], F32, tag="minus_skip")
             nc.vector.scalar_tensor_tensor(
-                out=by_tile(t), in0=by_tile(hsum[b]), scalar=0.0, in1=x_of(b), op0=ALU.max, op1=ALU.subtract
+                out=by_tile(t), in0=by_tile(hw_nodes[b]), scalar=1.0, in1=x_of(b), op0=ALU.subtract, op1=ALU.mult
             )
-            diff[b] = t
+            minus_skip[b] = t
 
         def finish_gate(b):
             t = work.tile([P, CHUNK], F32, tag="gated")
-            nc.vector.tensor_tensor(out=t[:], in0=hw_nodes[b][:], in1=diff[b][:], op=ALU.mult)
+            nc.vector.scalar_tensor_tensor(
+                out=t[:], in0=hsum[b][:], scalar=0.0, in1=hw_nodes[b][:], op0=ALU.max, op1=ALU.mult
+            )
             gated[b] = t
 
         def finish_out(b):
             tiles, feats = place(b)
             result = work.tile([P, CHUNK], F32, tag="result", bufs=3)
-            nc.vector.tensor_tensor(out=by_tile(result), in0=by_tile(gated[b]), in1=x_of(b), op=ALU.add)
+            nc.vector.tensor_tensor(out=result[:], in0=gated[b][:], in1=minus_skip[b][:], op=ALU.subtract)
             nc.sync.dma_start(out=out_view[:, tiles, feats], in_=by_tile(result))
 
         bias_rows32 = keep.tile([P, P], F32)
-        nc.vector.tensor_copy(out=bias_rows32[:], in_=bias_rows[:])
 
         def bias_columns():
             bias_flipped = psum.tile([P, P], F32, tag="node", bufs=3)
@@ -324,10 +332,12 @@ def tile_graphconvolution_pb_kernel(tc, agg, x, wih, whh, bih, bhh, wh, bh, out)
         waiting = []
         for i, unit in enumerate(first):
             waiting.append((unit, regroup(flip(unit), nc.vector.tensor_copy if i % 2 else nc.scalar.copy)))
-            if i == 3:
-                bias_columns()
             if len(waiting) > 1:
                 quantise(*waiting.pop(0))
+            if i == 3:
+                nc.vector.tensor_copy(out=bias_rows32[:], in_=bias_rows[:])
+            if i == 5:
+                bias_columns()
         quantise(*waiting.pop(0))
 
         units = []
@@ -340,15 +350,16 @@ def tile_graphconvolution_pb_kernel(tc, agg, x, wih, whh, bih, bhh, wh, bh, out)
             units.extend(node_units(agg_nat[:, d], agg_codes[:, d], agg_scales[:, d], 1))
 
         def share(i):
-            if i <= 0:
-                return 3 if i == 0 else 2
-            return 2 if i % DIRS == 2 else 1
+            if i == 0:
+                return 3
+            return 0 if i > 0 and i % DIRS == 1 else 2
 
         def ending(j):
             return j // DIRS if 0 <= j < STEPS and j % DIRS == DIRS - 1 else None
 
         copied = []
         for i in range(-2, STEPS + 4):
+            b1, b2, b3, b4 = [ending(i - n) for n in (1, 2, 3, 4)]
             if 0 <= i + 1 < STEPS:
                 products(i + 1)
             job = [units.pop(0) for n in range(min(share(i), len(units)))]
@@ -357,36 +368,31 @@ def tile_graphconvolution_pb_kernel(tc, agg, x, wih, whh, bih, bhh, wh, bh, out)
                 reset_hidden(i)
             if 0 <= i + 1 < STEPS:
                 gates(i + 1)
-            for b in [ending(i - 2)]:
-                if b is not None:
-                    finish_zh(b)
-            for b in [ending(i - 3)]:
-                if b is not None:
-                    finish_sum(b)
-            for b in [ending(i - 4)]:
-                if b is not None:
-                    finish_gate(b)
+            if b2 is not None:
+                finish_zh(b2)
+            if b3 is not None:
+                finish_sum(b3)
+            if b4 is not None:
+                finish_gate(b4)
             if 0 <= i < STEPS:
                 candidate_input(i)
                 candidate(i)
                 blend(i)
+            if 0 <= i + 1 < STEPS and (i + 1) % DIRS:
+                add_fresh(i + 1)
             copying = [(unit, regroup(fl, nc.scalar.copy)) for unit, fl in zip(job, flipped)]
             if i == 0:
                 wh_grouped = keep.tile([P, FEATS, PACK], BF16, align_bytes=64)
                 nc.vector.tensor_copy(out=wh_grouped[:], in_=wh_nat[:].rearrange("p t o -> p o t"))
-            for b in [ending(i - 3)]:
-                if b is not None:
-                    finish_diff(b)
-                    hw_nodes[b] = back_to_nodes([hw[b]])
-            for b in [ending(i - 4)]:
-                if b is not None:
-                    finish_out(b)
-            for b in [ending(i - 1)]:
-                if b is not None:
-                    fresh_sum[b] = back_to_nodes([fresh[b * DIRS + d] for d in range(DIRS)])
-            for b in [ending(i - 2)]:
-                if b is not None:
-                    part_sum[b] = back_to_nodes([part[b * DIRS + d] for d in range(DIRS)])
+            if b3 is not None:
+                finish_skip(b3)
+            if b4 is not None:
+                finish_out(b4)
+            if b1 is not None:
+                fresh_sum[b1] = back_to_nodes([fresh_total[b1 * DIRS + DIRS - 1]])
+            if b2 is not None:
+                part_sum[b2] = back_to_nodes([part[b2 * DIRS + d] for d in range(DIRS)])
+                hw_nodes[b2] = back_to_nodes([hw[b2]])
             for unit, grouped in copied:
                 quantise(unit, grouped)
             copied = copying

@@ -78,12 +78,14 @@ def tile_graphconvolution_pb_kernel(tc, agg, x, wih, whh, bih, bhh, wh, bh, out)
         warm = keep.tile([P, 1], F32)
         nc.vector.memset(warm[:], 0.0)
         nc.scalar.activation(out=warm[:], in_=warm[:], func=ACT.Sigmoid)
-        load_x(0)
         nc.sync.dma_start(out=bias_rows[BIH_R:BHH_R, :], in_=bih.rearrange("(r m) -> r m", m=P))
         nc.sync.dma_start(out=bias_rows[BHH_R:BH, :], in_=bhh.rearrange("(r m) -> r m", m=P))
         nc.sync.dma_start(out=bias_rows[BH : BH + FEAT_TILES, :], in_=bh.rearrange("(r m) -> r m", m=P))
+        load_x(0)
+        nc.sync.dma_start(out=w_nat[:, 0, HH_R : HH_N + 1, :], in_=whh_view[0])
         load_agg(0, 0)
-        load_weights(0)
+        nc.sync.dma_start(out=w_nat[:, 0, IH_R, :], in_=wih_view[0][:, 0, :])
+        nc.sync.dma_start(out=w_nat[:, 0, IH_Z : IH_N + 1, :], in_=wih_view[0][:, 1:, :])
         load_agg(1, 0)
         load_agg(2, 0)
         nc.sync.dma_start(
@@ -153,6 +155,7 @@ def tile_graphconvolution_pb_kernel(tc, agg, x, wih, whh, bih, bhh, wh, bh, out)
         hw = {}
         reset = {}
         fresh = {}
+        fresh_two = {}
         pre = {}
         cand = {}
         part = {}
@@ -162,7 +165,6 @@ def tile_graphconvolution_pb_kernel(tc, agg, x, wih, whh, bih, bhh, wh, bh, out)
         minus_zh = {}
         hsum = {}
         minus_skip = {}
-        fresh_total = {}
         gated = {}
 
         def weight_pass(acc, f, g, moving, start, stop):
@@ -176,81 +178,107 @@ def tile_graphconvolution_pb_kernel(tc, agg, x, wih, whh, bih, bhh, wh, bh, out)
                 stop=stop,
             )
 
-        def products(s):
+        def operands(s):
             b, d = divmod(s, DIRS)
             c, f = divmod(b, FEAT_TILES)
             nodes = slice(c * CHUNK, (c + 1) * CHUNK)
-            xq = (x_codes[:, nodes], x_scales[:, nodes])
-            aq = (agg_codes[:, d, nodes], agg_scales[:, d, nodes])
+            return b, d, f, (x_codes[:, nodes], x_scales[:, nodes]), (agg_codes[:, d, nodes], agg_scales[:, d, nodes])
+
+        def product_r(s):
+            b, d, f, xq, aq = operands(s)
             a_r = psum.tile([P, CHUNK], F32, tag="gate", bufs=4)
             weight_pass(a_r, f, IH_R, aq, True, False)
             weight_pass(a_r, f, HH_R, xq, False, True)
-            if d == 0:
-                h_n = psum.tile([P, CHUNK], F32, tag="hn", bufs=1)
-                weight_pass(h_n, f, HH_N, xq, True, True)
-                hid_n[b] = h_n
+            acc_r[s] = a_r
+
+        def product_z(s):
+            b, d, f, xq, aq = operands(s)
             a_z = psum.tile([P, CHUNK], F32, tag="gate", bufs=4)
             weight_pass(a_z, f, IH_Z, aq, True, False)
             weight_pass(a_z, f, HH_Z, xq, False, True)
+            acc_z[s] = a_z
+
+        def product_n(s):
+            b, d, f, xq, aq = operands(s)
             a_n = psum.tile([P, CHUNK], F32, tag="gate", bufs=4)
             weight_pass(a_n, f, IH_N, aq, True, True)
-            acc_r[s] = a_r
-            acc_z[s] = a_z
             acc_n[s] = a_n
-            if d == DIRS - 1:
-                feats = slice(f * P, (f + 1) * P)
-                a_hw = psum.tile([P, CHUNK], F32, tag="gate", bufs=4)
-                nc.tensor.matmul_mx(
-                    out=a_hw[:], lhsT=wh_codes[:, feats].bitcast(FP8X4), lhsT_scale=wh_scales[:, feats],
-                    rhs=xq[0].bitcast(FP8X4), rhs_scale=xq[1], start=True, stop=True,
-                )
-                hw_acc[b] = a_hw
 
-        def gates(s):
-            b, d = divmod(s, DIRS)
+        def product_hn(b):
             f = b % FEAT_TILES
-            r = work.tile([P, CHUNK], F32, tag="reset")
+            h_n = psum.tile([P, CHUNK], F32, tag="hn", bufs=1)
+            weight_pass(h_n, f, HH_N, operands(b * DIRS)[3], True, True)
+            hid_n[b] = h_n
+
+        def product_hw(b):
+            b, d, f, xq, aq = operands(b * DIRS)
+            feats = slice(f * P, (f + 1) * P)
+            a_hw = psum.tile([P, CHUNK], F32, tag="gate", bufs=4)
+            nc.tensor.matmul_mx(
+                out=a_hw[:], lhsT=wh_codes[:, feats].bitcast(FP8X4), lhsT_scale=wh_scales[:, feats],
+                rhs=xq[0].bitcast(FP8X4), rhs_scale=xq[1], start=True, stop=True,
+            )
+            hw_acc[b] = a_hw
+
+        def gate_r(s):
+            f = s // DIRS % FEAT_TILES
+            r = work.tile([P, CHUNK], F32, tag="reset", bufs=3)
             nc.scalar.activation(out=r[:], in_=acc_r[s][:], func=ACT.Sigmoid, bias=b_r[:, f : f + 1])
-            fr = work.tile([P, CHUNK], F32, tag="fresh", bufs=7)
+            reset[s] = r
+
+        def gate_z(s):
+            f = s // DIRS % FEAT_TILES
+            fr = work.tile([P, CHUNK], F32, tag="fresh", bufs=9)
             nc.scalar.activation(
                 out=fr[:], in_=acc_z[s][:], func=ACT.Sigmoid, bias=minus_b_z[:, f : f + 1], scale=-1.0
             )
-            reset[s] = r
             fresh[s] = fr
-            if d == DIRS - 1:
-                t = work.tile([P, CHUNK], F32, tag="hw")
-                nc.scalar.activation(out=t[:], in_=hw_acc[b][:], func=ACT.Relu, bias=bias_cols[:, BH + f : BH + f + 1])
-                hw[b] = t
+
+        def gate_hw(b):
+            f = b % FEAT_TILES
+            t = work.tile([P, CHUNK], F32, tag="hw", bufs=3)
+            nc.scalar.activation(out=t[:], in_=hw_acc[b][:], func=ACT.Relu, bias=bias_cols[:, BH + f : BH + f + 1])
+            hw[b] = t
+
+        def pieces(s):
+            return [slice(0, CHUNK // 2), slice(CHUNK // 2, CHUNK)] if s == STEPS - 1 else [slice(0, CHUNK)]
 
         def reset_hidden(s):
             b = s // DIRS
             f = b % FEAT_TILES
-            a = work.tile([P, CHUNK], F32, tag="pre")
-            nc.vector.scalar_tensor_tensor(
-                out=a[:], in0=hid_n[b][:], scalar=bias_cols[:, BHH_N + f : BHH_N + f + 1], in1=reset[s][:],
-                op0=ALU.add, op1=ALU.mult,
-            )
+            a = work.tile([P, CHUNK], F32, tag="pre", bufs=3)
+            for cols in pieces(s):
+                nc.vector.scalar_tensor_tensor(
+                    out=a[:, cols], in0=hid_n[b][:, cols], scalar=bias_cols[:, BHH_N + f : BHH_N + f + 1],
+                    in1=reset[s][:, cols], op0=ALU.add, op1=ALU.mult,
+                )
             pre[s] = a
 
         def candidate_input(s):
-            nc.vector.tensor_tensor(out=pre[s][:], in0=acc_n[s][:], in1=pre[s][:], op=ALU.add)
+            a = pre[s]
+            for cols in pieces(s):
+                nc.vector.tensor_tensor(out=a[:, cols], in0=acc_n[s][:, cols], in1=a[:, cols], op=ALU.add)
 
         def candidate(s):
-            f = (s // DIRS) % FEAT_TILES
-            cd = work.tile([P, CHUNK], F32, tag="cand")
-            nc.scalar.activation(out=cd[:], in_=pre[s][:], func=ACT.Tanh, bias=bias_cols[:, BIH_N + f : BIH_N + f + 1])
+            f = s // DIRS % FEAT_TILES
+            cd = work.tile([P, CHUNK], F32, tag="cand", bufs=3)
+            for cols in pieces(s):
+                nc.scalar.activation(
+                    out=cd[:, cols], in_=pre[s][:, cols], func=ACT.Tanh, bias=bias_cols[:, BIH_N + f : BIH_N + f + 1]
+                )
             cand[s] = cd
 
         def blend(s):
-            pt = work.tile([P, CHUNK], F32, tag="part", bufs=7)
-            nc.gpsimd.tensor_tensor(out=pt[:], in0=fresh[s][:], in1=cand[s][:], op=ALU.mult)
+            pt = work.tile([P, CHUNK], F32, tag="part", bufs=9)
+            engine = nc.vector if s == STEPS - 1 else nc.gpsimd
+            for cols in pieces(s):
+                engine.tensor_tensor(out=pt[:, cols], in0=fresh[s][:, cols], in1=cand[s][:, cols], op=ALU.mult)
             part[s] = pt
 
         def add_fresh(s):
-            t = work.tile([P, CHUNK], F32, tag="fresh_total", bufs=3)
-            before = fresh[s - 1] if s % DIRS == 1 else fresh_total[s - 1]
-            nc.gpsimd.tensor_tensor(out=t[:], in0=before[:], in1=fresh[s][:], op=ALU.add)
-            fresh_total[s] = t
+            t = work.tile([P, CHUNK], F32, tag="fresh_two")
+            nc.gpsimd.tensor_tensor(out=t[:], in0=fresh[s - 1][:], in1=fresh[s][:], op=ALU.add)
+            fresh_two[s // DIRS] = t
 
         def back_to_nodes(terms):
             total = psum.tile([P, CHUNK], F32, tag="node", bufs=3)
@@ -262,6 +290,16 @@ def tile_graphconvolution_pb_kernel(tc, agg, x, wih, whh, bih, bhh, wh, bh, out)
                         start=(i == 0), stop=(i == len(terms) - 1),
                     )
             return total
+
+        def turn_fresh(b):
+            last = b * DIRS + DIRS - 1
+            fresh_sum[b] = back_to_nodes([fresh_two[b], fresh[last]])
+
+        def turn_part(b):
+            part_sum[b] = back_to_nodes([part[b * DIRS + d] for d in range(DIRS)])
+
+        def turn_hw(b):
+            hw_nodes[b] = back_to_nodes([hw[b]])
 
         def by_tile(t):
             return t[:].rearrange("p (j m) -> p j m", j=CHUNK_TILES)
@@ -284,7 +322,10 @@ def tile_graphconvolution_pb_kernel(tc, agg, x, wih, whh, bih, bhh, wh, bh, out)
 
         def finish_sum(b):
             t = work.tile([P, CHUNK], F32, tag="hsum")
-            nc.vector.tensor_tensor(out=t[:], in0=part_sum[b][:], in1=minus_zh[b][:], op=ALU.subtract)
+            for cols in pieces(b * DIRS + DIRS - 1):
+                nc.vector.tensor_tensor(
+                    out=t[:, cols], in0=part_sum[b][:, cols], in1=minus_zh[b][:, cols], op=ALU.subtract
+                )
             hsum[b] = t
 
         def finish_skip(b):
@@ -296,20 +337,27 @@ def tile_graphconvolution_pb_kernel(tc, agg, x, wih, whh, bih, bhh, wh, bh, out)
 
         def finish_gate(b):
             t = work.tile([P, CHUNK], F32, tag="gated")
-            nc.vector.scalar_tensor_tensor(
-                out=t[:], in0=hsum[b][:], scalar=0.0, in1=hw_nodes[b][:], op0=ALU.max, op1=ALU.mult
-            )
+            for cols in pieces(b * DIRS + DIRS - 1):
+                nc.vector.scalar_tensor_tensor(
+                    out=t[:, cols], in0=hsum[b][:, cols], scalar=0.0, in1=hw_nodes[b][:, cols],
+                    op0=ALU.max, op1=ALU.mult,
+                )
             gated[b] = t
 
         def finish_out(b):
             tiles, feats = place(b)
             result = work.tile([P, CHUNK], F32, tag="result", bufs=3)
-            nc.vector.tensor_tensor(out=result[:], in0=gated[b][:], in1=minus_skip[b][:], op=ALU.subtract)
-            nc.sync.dma_start(out=out_view[:, tiles, feats], in_=by_tile(result))
+            for cols in pieces(b * DIRS + DIRS - 1):
+                nc.vector.tensor_tensor(out=result[:, cols], in0=gated[b][:, cols], in1=minus_skip[b][:, cols], op=ALU.subtract)
+                some = slice(tiles.start + cols.start // P, tiles.start + cols.stop // P)
+                nc.sync.dma_start(
+                    out=out_view[:, some, feats], in_=result[:, cols].rearrange("p (j m) -> p j m", m=P)
+                )
 
         bias_rows32 = keep.tile([P, P], F32)
 
         def bias_columns():
+            nc.vector.tensor_copy(out=bias_rows32[:], in_=bias_rows[:])
             bias_flipped = psum.tile([P, P], F32, tag="node", bufs=3)
             nc.tensor.transpose(bias_flipped[:], bias_rows32[:], ident[:])
             nc.vector.tensor_copy(out=bias_cols[:], in_=bias_flipped[:, 0:32])
@@ -327,17 +375,16 @@ def tile_graphconvolution_pb_kernel(tc, agg, x, wih, whh, bih, bhh, wh, bh, out)
         minus_b_z = keep.tile([P, FEAT_TILES], F32)
 
         first = node_units(x_nat, x_codes, x_scales, 0)
+        weights = weight_units(0)
+        first.append(weights[0])
         first.extend(node_units(agg_nat[:, 0], agg_codes[:, 0], agg_scales[:, 0], 0))
-        first.extend(weight_units(0))
+        first.extend(weights[1:])
+        bias_columns()
         waiting = []
         for i, unit in enumerate(first):
             waiting.append((unit, regroup(flip(unit), nc.vector.tensor_copy if i % 2 else nc.scalar.copy)))
             if len(waiting) > 1:
                 quantise(*waiting.pop(0))
-            if i == 3:
-                nc.vector.tensor_copy(out=bias_rows32[:], in_=bias_rows[:])
-            if i == 5:
-                bias_columns()
         quantise(*waiting.pop(0))
 
         units = []
@@ -357,42 +404,43 @@ def tile_graphconvolution_pb_kernel(tc, agg, x, wih, whh, bih, bhh, wh, bh, out)
         def ending(j):
             return j // DIRS if 0 <= j < STEPS and j % DIRS == DIRS - 1 else None
 
+        def step(stage, s):
+            if 0 <= s < STEPS:
+                stage(s)
+
+        def block(stage, s):
+            if 0 <= s < STEPS and s % DIRS == DIRS - 1:
+                stage(s // DIRS)
+
         copied = []
-        for i in range(-2, STEPS + 4):
-            b1, b2, b3, b4 = [ending(i - n) for n in (1, 2, 3, 4)]
-            if 0 <= i + 1 < STEPS:
-                products(i + 1)
+        for i in range(-2, STEPS + 6):
+            step(product_r, i + 1)
+            block(product_hn, i + 3)
+            step(product_z, i + 1)
+            step(product_n, i + 1)
+            block(product_hw, i + 1)
             job = [units.pop(0) for n in range(min(share(i), len(units)))]
             flipped = [flip(unit) for unit in job]
-            if 0 <= i < STEPS:
-                reset_hidden(i)
-            if 0 <= i + 1 < STEPS:
-                gates(i + 1)
-            if b2 is not None:
-                finish_zh(b2)
-            if b3 is not None:
-                finish_sum(b3)
-            if b4 is not None:
-                finish_gate(b4)
-            if 0 <= i < STEPS:
-                candidate_input(i)
-                candidate(i)
-                blend(i)
-            if 0 <= i + 1 < STEPS and (i + 1) % DIRS:
-                add_fresh(i + 1)
+            step(reset_hidden, i)
+            step(gate_r, i + 1)
+            step(gate_z, i + 1)
+            block(gate_hw, i + 1)
+            block(finish_zh, i - 2)
+            block(finish_sum, i - 3)
+            block(finish_gate, i - 4)
+            step(candidate_input, i)
+            step(candidate, i)
+            step(blend, i)
+            if (i + 1) % DIRS == 1:
+                step(add_fresh, i + 1)
             copying = [(unit, regroup(fl, nc.scalar.copy)) for unit, fl in zip(job, flipped)]
             if i == 0:
                 wh_grouped = keep.tile([P, FEATS, PACK], BF16, align_bytes=64)
                 nc.vector.tensor_copy(out=wh_grouped[:], in_=wh_nat[:].rearrange("p t o -> p o t"))
-            if b3 is not None:
-                finish_skip(b3)
-            if b4 is not None:
-                finish_out(b4)
-            if b1 is not None:
-                fresh_sum[b1] = back_to_nodes([fresh_total[b1 * DIRS + DIRS - 1]])
-            if b2 is not None:
-                part_sum[b2] = back_to_nodes([part[b2 * DIRS + d] for d in range(DIRS)])
-                hw_nodes[b2] = back_to_nodes([hw[b2]])
+            block(finish_skip, i - 3)
+            block(turn_fresh, i - 1)
+            block(turn_part, i - 2)
+            block(turn_hw, i - 2)
             for unit, grouped in copied:
                 quantise(unit, grouped)
             copied = copying
@@ -401,3 +449,4 @@ def tile_graphconvolution_pb_kernel(tc, agg, x, wih, whh, bih, bhh, wh, bh, out)
                     out=wh_codes[:].bitcast(FP8X4), scales=wh_scales[:],
                     in_=wh_grouped[:].rearrange("p o t -> p (o t)"),
                 )
+            block(finish_out, i - 5)

@@ -78,10 +78,10 @@ def tile_graphconvolution_pb_kernel(tc, agg, x, wih, whh, bih, bhh, wh, bh, out)
         warm = keep.tile([P, 1], F32)
         nc.vector.memset(warm[:], 0.0)
         nc.scalar.activation(out=warm[:], in_=warm[:], func=ACT.Sigmoid)
+        load_x(0)
         nc.sync.dma_start(out=bias_rows[BIH_R:BHH_R, :], in_=bih.rearrange("(r m) -> r m", m=P))
         nc.sync.dma_start(out=bias_rows[BHH_R:BH, :], in_=bhh.rearrange("(r m) -> r m", m=P))
         nc.sync.dma_start(out=bias_rows[BH : BH + FEAT_TILES, :], in_=bh.rearrange("(r m) -> r m", m=P))
-        load_x(0)
         nc.sync.dma_start(out=w_nat[:, 0, HH_R : HH_N + 1, :], in_=whh_view[0])
         load_agg(0, 0)
         nc.sync.dma_start(out=w_nat[:, 0, IH_R, :], in_=wih_view[0][:, 0, :])
@@ -209,6 +209,21 @@ def tile_graphconvolution_pb_kernel(tc, agg, x, wih, whh, bih, bhh, wh, bh, out)
             h_n = psum.tile([P, CHUNK], F32, tag="hn", bufs=1)
             weight_pass(h_n, f, HH_N, operands(b * DIRS)[3], True, True)
             hid_n[b] = h_n
+
+        def copy_wh(b):
+            if b < FEAT_TILES:
+                cols = slice(b * P, (b + 1) * P)
+                nc.vector.tensor_copy(out=wh_grouped[:, cols, :], in_=wh_nat[:, :, cols].rearrange("p t o -> p o t"))
+
+        def quantise_wh(b):
+            if b < FEAT_TILES:
+                cols = slice(b * P, (b + 1) * P)
+                nc.vector.quantize_mx(
+                    out=wh_codes[:, cols].bitcast(FP8X4), scales=wh_scales[:, cols],
+                    in_=wh_grouped[:, cols, :].rearrange("p o t -> p (o t)"),
+                )
+
+        wh_grouped = keep.tile([P, FEATS, PACK], BF16, align_bytes=64)
 
         def product_hw(b):
             b, d, f, xq, aq = operands(b * DIRS)
@@ -357,7 +372,6 @@ def tile_graphconvolution_pb_kernel(tc, agg, x, wih, whh, bih, bhh, wh, bh, out)
         bias_rows32 = keep.tile([P, P], F32)
 
         def bias_columns():
-            nc.vector.tensor_copy(out=bias_rows32[:], in_=bias_rows[:])
             bias_flipped = psum.tile([P, P], F32, tag="node", bufs=3)
             nc.tensor.transpose(bias_flipped[:], bias_rows32[:], ident[:])
             nc.vector.tensor_copy(out=bias_cols[:], in_=bias_flipped[:, 0:32])
@@ -379,12 +393,15 @@ def tile_graphconvolution_pb_kernel(tc, agg, x, wih, whh, bih, bhh, wh, bh, out)
         first.append(weights[0])
         first.extend(node_units(agg_nat[:, 0], agg_codes[:, 0], agg_scales[:, 0], 0))
         first.extend(weights[1:])
-        bias_columns()
         waiting = []
         for i, unit in enumerate(first):
             waiting.append((unit, regroup(flip(unit), nc.vector.tensor_copy if i % 2 else nc.scalar.copy)))
             if len(waiting) > 1:
                 quantise(*waiting.pop(0))
+            if i == 0:
+                nc.scalar.copy(out=bias_rows32[:], in_=bias_rows[:])
+            if i == 3:
+                bias_columns()
         quantise(*waiting.pop(0))
 
         units = []
@@ -422,21 +439,23 @@ def tile_graphconvolution_pb_kernel(tc, agg, x, wih, whh, bih, bhh, wh, bh, out)
             job = [units.pop(0) for n in range(min(share(i), len(units)))]
             flipped = [flip(unit) for unit in job]
             step(reset_hidden, i)
+            if i == STEPS - 1:
+                candidate_input(i)
+                candidate(i)
             step(gate_r, i + 1)
             step(gate_z, i + 1)
             block(gate_hw, i + 1)
             block(finish_zh, i - 2)
             block(finish_sum, i - 3)
             block(finish_gate, i - 4)
-            step(candidate_input, i)
-            step(candidate, i)
+            if i < STEPS - 1:
+                step(candidate_input, i)
+                step(candidate, i)
             step(blend, i)
             if (i + 1) % DIRS == 1:
                 step(add_fresh, i + 1)
             copying = [(unit, regroup(fl, nc.scalar.copy)) for unit, fl in zip(job, flipped)]
-            if i == 0:
-                wh_grouped = keep.tile([P, FEATS, PACK], BF16, align_bytes=64)
-                nc.vector.tensor_copy(out=wh_grouped[:], in_=wh_nat[:].rearrange("p t o -> p o t"))
+            block(copy_wh, i + 3)
             block(finish_skip, i - 3)
             block(turn_fresh, i - 1)
             block(turn_part, i - 2)
@@ -444,9 +463,5 @@ def tile_graphconvolution_pb_kernel(tc, agg, x, wih, whh, bih, bhh, wh, bh, out)
             for unit, grouped in copied:
                 quantise(unit, grouped)
             copied = copying
-            if i == 0:
-                nc.vector.quantize_mx(
-                    out=wh_codes[:].bitcast(FP8X4), scales=wh_scales[:],
-                    in_=wh_grouped[:].rearrange("p o t -> p (o t)"),
-                )
+            block(quantise_wh, i + 2)
             block(finish_out, i - 5)

@@ -75,6 +75,8 @@ def tile_graphconvolution_pb_kernel(tc, agg, x, wih, whh, bih, bhh, wh, bh, out)
             nc.sync.dma_start(out=w_nat[:, f, IH_R : IH_N + 1, :], in_=wih_view[f])
 
         nc.vector.memset(bias_rows[:], 0.0)
+        zeros = keep.tile([P, CHUNK], BF16)
+        nc.vector.memset(zeros[:], 0.0)
         warm = keep.tile([P, 1], F32)
         nc.vector.memset(warm[:], 0.0)
         nc.scalar.activation(out=warm[:], in_=warm[:], func=ACT.Sigmoid)
@@ -393,8 +395,17 @@ def tile_graphconvolution_pb_kernel(tc, agg, x, wih, whh, bih, bhh, wh, bh, out)
         first.append(weights[0])
         first.extend(node_units(agg_nat[:, 0], agg_codes[:, 0], agg_scales[:, 0], 0))
         first.extend(weights[1:])
+        idle = psum.tile([P, CHUNK], F32, tag="hn", bufs=1)
+
+        def keep_busy(count):
+            for n in range(count):
+                nc.tensor.matmul(out=idle[:], lhsT=zeros[:, 0:P], rhs=zeros[:], start=True, stop=True)
+
+        keep_busy(5)
         waiting = []
         for i, unit in enumerate(first):
+            if i > 0:
+                keep_busy(2)
             waiting.append((unit, regroup(flip(unit), nc.vector.tensor_copy if i % 2 else nc.scalar.copy)))
             if len(waiting) > 1:
                 quantise(*waiting.pop(0))

@@ -131,9 +131,9 @@ def tile_graphconvolution_pb_kernel(tc, agg, x, wih, whh, bih, bhh, wh, bh, out)
                 )
             return units
 
-        def flip(unit):
+        def flip(unit, tag="node", bufs=3):
             words = unit[0].bitcast(F32)
-            flipped = psum.tile([P, 2, 2, P], F32, tag="node", bufs=3)
+            flipped = psum.tile([P, 2, 2, P], F32, tag=tag, bufs=bufs)
             for i in range(2):
                 for u in range(2):
                     nc.tensor.transpose(flipped[:, i, u, :], words[:, i, u * P : (u + 1) * P], ident[:])
@@ -297,8 +297,8 @@ def tile_graphconvolution_pb_kernel(tc, agg, x, wih, whh, bih, bhh, wh, bh, out)
             nc.gpsimd.tensor_tensor(out=t[:], in0=fresh[s - 1][:], in1=fresh[s][:], op=ALU.add)
             fresh_two[s // DIRS] = t
 
-        def back_to_nodes(terms):
-            total = psum.tile([P, CHUNK], F32, tag="node", bufs=3)
+        def back_to_nodes(terms, tag="node", bufs=3):
+            total = psum.tile([P, CHUNK], F32, tag=tag, bufs=bufs)
             for j in range(CHUNK_TILES):
                 cols = slice(j * P, (j + 1) * P)
                 for i, term in enumerate(terms):
@@ -312,11 +312,11 @@ def tile_graphconvolution_pb_kernel(tc, agg, x, wih, whh, bih, bhh, wh, bh, out)
             last = b * DIRS + DIRS - 1
             fresh_sum[b] = back_to_nodes([fresh_two[b], fresh[last]])
 
-        def turn_part(b):
-            part_sum[b] = back_to_nodes([part[b * DIRS + d] for d in range(DIRS)])
+        def turn_part(b, *bank):
+            part_sum[b] = back_to_nodes([part[b * DIRS + d] for d in range(DIRS)], *bank)
 
-        def turn_hw(b):
-            hw_nodes[b] = back_to_nodes([hw[b]])
+        def turn_hw(b, *bank):
+            hw_nodes[b] = back_to_nodes([hw[b]], *bank)
 
         def by_tile(t):
             return t[:].rearrange("p (j m) -> p j m", j=CHUNK_TILES)
@@ -346,14 +346,14 @@ def tile_graphconvolution_pb_kernel(tc, agg, x, wih, whh, bih, bhh, wh, bh, out)
             hsum[b] = t
 
         def finish_skip(b):
-            t = work.tile([P, CHUNK], F32, tag="minus_skip")
+            t = work.tile([P, CHUNK], F32, tag="minus_skip", bufs=3)
             nc.vector.scalar_tensor_tensor(
                 out=by_tile(t), in0=by_tile(hw_nodes[b]), scalar=1.0, in1=x_of(b), op0=ALU.subtract, op1=ALU.mult
             )
             minus_skip[b] = t
 
         def finish_gate(b):
-            t = work.tile([P, CHUNK], F32, tag="gated")
+            t = work.tile([P, CHUNK], F32, tag="gated", bufs=3)
             for cols in pieces(b * DIRS + DIRS - 1):
                 nc.vector.scalar_tensor_tensor(
                     out=t[:, cols], in0=hsum[b][:, cols], scalar=0.0, in1=hw_nodes[b][:, cols],
@@ -361,11 +361,13 @@ def tile_graphconvolution_pb_kernel(tc, agg, x, wih, whh, bih, bhh, wh, bh, out)
                 )
             gated[b] = t
 
-        def finish_out(b):
+        def finish_out(b, engine=nc.vector):
             tiles, feats = place(b)
             result = work.tile([P, CHUNK], F32, tag="result", bufs=3)
             for cols in pieces(b * DIRS + DIRS - 1):
-                nc.vector.tensor_tensor(out=result[:, cols], in0=gated[b][:, cols], in1=minus_skip[b][:, cols], op=ALU.subtract)
+                engine.tensor_tensor(
+                    out=result[:, cols], in0=gated[b][:, cols], in1=minus_skip[b][:, cols], op=ALU.subtract
+                )
                 some = slice(tiles.start + cols.start // P, tiles.start + cols.stop // P)
                 nc.sync.dma_start(
                     out=out_view[:, some, feats], in_=result[:, cols].rearrange("p (j m) -> p j m", m=P)
@@ -405,8 +407,9 @@ def tile_graphconvolution_pb_kernel(tc, agg, x, wih, whh, bih, bhh, wh, bh, out)
         waiting = []
         for i, unit in enumerate(first):
             if i > 0:
-                keep_busy(2)
-            waiting.append((unit, regroup(flip(unit), nc.vector.tensor_copy if i % 2 else nc.scalar.copy)))
+                keep_busy(1)
+            flipped = flip(unit, "gate", 4) if i < 4 else flip(unit)
+            waiting.append((unit, regroup(flipped, nc.vector.tensor_copy if i in (1, 4) else nc.scalar.copy)))
             if len(waiting) > 1:
                 quantise(*waiting.pop(0))
             if i == 0:
@@ -441,7 +444,7 @@ def tile_graphconvolution_pb_kernel(tc, agg, x, wih, whh, bih, bhh, wh, bh, out)
                 stage(s // DIRS)
 
         copied = []
-        for i in range(-2, STEPS + 6):
+        for i in range(-2, STEPS - 1):
             step(product_r, i + 1)
             block(product_hn, i + 3)
             step(product_z, i + 1)
@@ -450,18 +453,15 @@ def tile_graphconvolution_pb_kernel(tc, agg, x, wih, whh, bih, bhh, wh, bh, out)
             job = [units.pop(0) for n in range(min(share(i), len(units)))]
             flipped = [flip(unit) for unit in job]
             step(reset_hidden, i)
-            if i == STEPS - 1:
-                candidate_input(i)
-                candidate(i)
             step(gate_r, i + 1)
             step(gate_z, i + 1)
-            block(gate_hw, i + 1)
+            if i < STEPS - 2:
+                block(gate_hw, i + 1)
             block(finish_zh, i - 2)
             block(finish_sum, i - 3)
             block(finish_gate, i - 4)
-            if i < STEPS - 1:
-                step(candidate_input, i)
-                step(candidate, i)
+            step(candidate_input, i)
+            step(candidate, i)
             step(blend, i)
             if (i + 1) % DIRS == 1:
                 step(add_fresh, i + 1)
@@ -475,4 +475,26 @@ def tile_graphconvolution_pb_kernel(tc, agg, x, wih, whh, bih, bhh, wh, bh, out)
                 quantise(unit, grouped)
             copied = copying
             block(quantise_wh, i + 2)
-            block(finish_out, i - 5)
+            if i < STEPS - 2:
+                block(finish_out, i - 5)
+
+        last = STEPS - 1
+        before, end = BLOCKS - 2, BLOCKS - 1
+        reset_hidden(last)
+        candidate_input(last)
+        gate_hw(end)
+        candidate(last)
+        finish_out(end - 2, nc.gpsimd)
+        turn_fresh(end)
+        turn_hw(end, "gate", 4)
+        finish_sum(before)
+        finish_skip(before)
+        blend(last)
+        turn_part(end, "gate", 4)
+        finish_skip(end)
+        finish_zh(end)
+        finish_gate(before)
+        finish_out(before, nc.gpsimd)
+        finish_sum(end)
+        finish_gate(end)
+        finish_out(end)

@@ -361,7 +361,7 @@ def tile_graphconvolution_pb_kernel(tc, agg, x, wih, whh, bih, bhh, wh, bh, out)
                 )
             gated[b] = t
 
-        def finish_out(b, engine=nc.vector):
+        def finish_out(b, engine=nc.vector, queue=nc.sync):
             tiles, feats = place(b)
             result = work.tile([P, CHUNK], F32, tag="result", bufs=3)
             for cols in pieces(b * DIRS + DIRS - 1):
@@ -369,7 +369,7 @@ def tile_graphconvolution_pb_kernel(tc, agg, x, wih, whh, bih, bhh, wh, bh, out)
                     out=result[:, cols], in0=gated[b][:, cols], in1=minus_skip[b][:, cols], op=ALU.subtract
                 )
                 some = slice(tiles.start + cols.start // P, tiles.start + cols.stop // P)
-                nc.sync.dma_start(
+                queue.dma_start(
                     out=out_view[:, some, feats], in_=result[:, cols].rearrange("p (j m) -> p j m", m=P)
                 )
 
@@ -397,9 +397,8 @@ def tile_graphconvolution_pb_kernel(tc, agg, x, wih, whh, bih, bhh, wh, bh, out)
         first.append(weights[0])
         first.extend(node_units(agg_nat[:, 0], agg_codes[:, 0], agg_scales[:, 0], 0))
         first.extend(weights[1:])
-        idle = psum.tile([P, CHUNK], F32, tag="hn", bufs=1)
-
         def keep_busy(count):
+            idle = psum.tile([P, CHUNK], F32, tag="hn", bufs=1)
             for n in range(count):
                 nc.tensor.matmul(out=idle[:], lhsT=zeros[:, 0:P], rhs=zeros[:], start=True, stop=True)
 
@@ -484,9 +483,11 @@ def tile_graphconvolution_pb_kernel(tc, agg, x, wih, whh, bih, bhh, wh, bh, out)
         candidate_input(last)
         gate_hw(end)
         candidate(last)
-        finish_out(end - 2, nc.gpsimd)
-        turn_fresh(end)
+        finish_out(end - 2, nc.gpsimd, nc.scalar)
+        keep_busy(2)
         turn_hw(end, "gate", 4)
+        turn_fresh(end)
+        keep_busy(2)
         finish_sum(before)
         finish_skip(before)
         blend(last)
@@ -494,7 +495,7 @@ def tile_graphconvolution_pb_kernel(tc, agg, x, wih, whh, bih, bhh, wh, bh, out)
         finish_skip(end)
         finish_zh(end)
         finish_gate(before)
-        finish_out(before, nc.gpsimd)
+        finish_out(before, nc.gpsimd, nc.scalar)
         finish_sum(end)
         finish_gate(end)
         finish_out(end)

@@ -79,13 +79,16 @@ def tile_graphconvolution_pb_kernel(tc, agg, x, wih, whh, bih, bhh, wh, bh, out)
         nc.vector.memset(zeros[:], 0.0)
         warm = keep.tile([P, 1], F32)
         nc.vector.memset(warm[:], 0.0)
+        nc.scalar.dma_start(out=bias_rows[BIH_R:BHH_R, :], in_=bih.rearrange("(r m) -> r m", m=P))
+        nc.scalar.dma_start(out=bias_rows[BHH_R:BH, :], in_=bhh.rearrange("(r m) -> r m", m=P))
+        nc.scalar.dma_start(out=bias_rows[BH : BH + FEAT_TILES, :], in_=bh.rearrange("(r m) -> r m", m=P))
         nc.scalar.activation(out=warm[:], in_=warm[:], func=ACT.Sigmoid)
-        load_x(0)
-        nc.sync.dma_start(out=bias_rows[BIH_R:BHH_R, :], in_=bih.rearrange("(r m) -> r m", m=P))
-        nc.sync.dma_start(out=bias_rows[BHH_R:BH, :], in_=bhh.rearrange("(r m) -> r m", m=P))
-        nc.sync.dma_start(out=bias_rows[BH : BH + FEAT_TILES, :], in_=bh.rearrange("(r m) -> r m", m=P))
+        half = CHUNK_TILES // 2
+        for tiles in (slice(0, half), slice(half, CHUNK_TILES)):
+            nc.sync.dma_start(out=x_nat[:, tiles, :], in_=x_view[:, tiles, :])
         nc.sync.dma_start(out=w_nat[:, 0, HH_R : HH_N + 1, :], in_=whh_view[0])
-        load_agg(0, 0)
+        for tiles in (slice(0, half), slice(half, CHUNK_TILES)):
+            nc.sync.dma_start(out=agg_nat[:, 0, tiles, :], in_=agg_view[0][:, tiles, :])
         nc.sync.dma_start(out=w_nat[:, 0, IH_R, :], in_=wih_view[0][:, 0, :])
         nc.sync.dma_start(out=w_nat[:, 0, IH_Z : IH_N + 1, :], in_=wih_view[0][:, 1:, :])
         load_agg(1, 0)
@@ -405,17 +408,18 @@ def tile_graphconvolution_pb_kernel(tc, agg, x, wih, whh, bih, bhh, wh, bh, out)
         keep_busy(5)
         waiting = []
         for i, unit in enumerate(first):
-            if i > 0:
-                keep_busy(1)
+            if i in (2, 3, 5, 6):
+                keep_busy(2)
             flipped = flip(unit, "gate", 4) if i < 4 else flip(unit)
             waiting.append((unit, regroup(flipped, nc.vector.tensor_copy if i in (1, 4) else nc.scalar.copy)))
             if len(waiting) > 1:
                 quantise(*waiting.pop(0))
-            if i == 0:
+            if i == 2:
                 nc.scalar.copy(out=bias_rows32[:], in_=bias_rows[:])
-            if i == 3:
+            if i == 5:
                 bias_columns()
         quantise(*waiting.pop(0))
+        keep_busy(1)
 
         units = []
         for d in range(1, DIRS):
@@ -465,7 +469,6 @@ def tile_graphconvolution_pb_kernel(tc, agg, x, wih, whh, bih, bhh, wh, bh, out)
             if (i + 1) % DIRS == 1:
                 step(add_fresh, i + 1)
             copying = [(unit, regroup(fl, nc.scalar.copy)) for unit, fl in zip(job, flipped)]
-            block(copy_wh, i + 3)
             block(finish_skip, i - 3)
             block(turn_fresh, i - 1)
             block(turn_part, i - 2)
@@ -473,6 +476,7 @@ def tile_graphconvolution_pb_kernel(tc, agg, x, wih, whh, bih, bhh, wh, bh, out)
             for unit, grouped in copied:
                 quantise(unit, grouped)
             copied = copying
+            block(copy_wh, i + 3)
             block(quantise_wh, i + 2)
             if i < STEPS - 2:
                 block(finish_out, i - 5)

@@ -74,15 +74,15 @@ def tile_graphconvolution_pb_kernel(tc, agg, x, wih, whh, bih, bhh, wh, bh, out)
             nc.sync.dma_start(out=w_nat[:, f, HH_R : HH_N + 1, :], in_=whh_view[f])
             nc.sync.dma_start(out=w_nat[:, f, IH_R : IH_N + 1, :], in_=wih_view[f])
 
-        nc.vector.memset(bias_rows[:], 0.0)
         zeros = keep.tile([P, CHUNK], BF16)
         nc.vector.memset(zeros[:], 0.0)
         warm = keep.tile([P, 1], F32)
         nc.vector.memset(warm[:], 0.0)
+        nc.vector.memset(bias_rows[:], 0.0)
+        nc.scalar.activation(out=warm[:], in_=warm[:], func=ACT.Sigmoid)
         nc.scalar.dma_start(out=bias_rows[BIH_R:BHH_R, :], in_=bih.rearrange("(r m) -> r m", m=P))
         nc.scalar.dma_start(out=bias_rows[BHH_R:BH, :], in_=bhh.rearrange("(r m) -> r m", m=P))
         nc.scalar.dma_start(out=bias_rows[BH : BH + FEAT_TILES, :], in_=bh.rearrange("(r m) -> r m", m=P))
-        nc.scalar.activation(out=warm[:], in_=warm[:], func=ACT.Sigmoid)
         half = CHUNK_TILES // 2
         for tiles in (slice(0, half), slice(half, CHUNK_TILES)):
             nc.sync.dma_start(out=x_nat[:, tiles, :], in_=x_view[:, tiles, :])
@@ -405,7 +405,7 @@ def tile_graphconvolution_pb_kernel(tc, agg, x, wih, whh, bih, bhh, wh, bh, out)
             for n in range(count):
                 nc.tensor.matmul(out=idle[:], lhsT=zeros[:, 0:P], rhs=zeros[:], start=True, stop=True)
 
-        keep_busy(5)
+        keep_busy(4)
         waiting = []
         for i, unit in enumerate(first):
             if i in (2, 3, 5, 6):
@@ -488,18 +488,18 @@ def tile_graphconvolution_pb_kernel(tc, agg, x, wih, whh, bih, bhh, wh, bh, out)
         gate_hw(end)
         candidate(last)
         finish_out(end - 2, nc.gpsimd, nc.scalar)
-        keep_busy(2)
         turn_hw(end, "gate", 4)
+        keep_busy(2)
         turn_fresh(end)
         keep_busy(2)
         finish_sum(before)
         finish_skip(before)
         blend(last)
         turn_part(end, "gate", 4)
-        finish_skip(end)
-        finish_zh(end)
         finish_gate(before)
         finish_out(before, nc.gpsimd, nc.scalar)
+        finish_zh(end)
+        finish_skip(end)
         finish_sum(end)
         finish_gate(end)
         finish_out(end)

from contextlib import ExitStack

import concourse.mybir as mybir
from concourse.masks import make_identity

F32 = mybir.dt.float32
BF16 = mybir.dt.bfloat16
U32 = mybir.dt.uint32
U8 = mybir.dt.uint8
FP8X4 = mybir.dt.float8_e4m3fn_x4
ACT = mybir.ActivationFunctionType
ALU = mybir.AluOpType

P = 128
PACK = 4
K = P * PACK
DIRS = 3
NODES = 1024
FEATS = 512
NODE_TILES = NODES // P
FEAT_TILES = FEATS // P
CHUNK_TILES = 4
CHUNK = CHUNK_TILES * P
CHUNKS = NODE_TILES // CHUNK_TILES
BLOCKS = CHUNKS * FEAT_TILES
STEPS = BLOCKS * DIRS
HH_R = 0
HH_Z = 1
HH_N = 2
IH_R = 3
IH_Z = 4
IH_N = 5
BIH_R = 0
BIH_Z = 4
BIH_N = 8
BHH_R = 12
BHH_Z = 16
BHH_N = 20
BH = 24

FLOPS = 2 * K * NODES * (DIRS * 3 * FEATS + 3 * FEATS + FEATS)


def tile_graphconvolution_pb_kernel(tc, agg, x, wih, whh, bih, bhh, wh, bh, out):
    nc = tc.nc
    with ExitStack() as stack:
        keep = stack.enter_context(tc.tile_pool(name="keep", bufs=1))
        work = stack.enter_context(tc.tile_pool(name="work", bufs=2))
        psum = stack.enter_context(tc.psum_pool(name="psum", bufs=1))
        stack.enter_context(tc.manual_schedule())

        x_nat = keep.tile([P, NODE_TILES, FEATS], BF16)
        agg_nat = keep.tile([P, DIRS, NODE_TILES, FEATS], BF16)
        w_nat = keep.tile([P, FEAT_TILES, 6, K], BF16)
        wh_nat = keep.tile([P, PACK, FEATS], BF16)
        bias_rows = keep.tile([P, P], BF16)

        x_view = x.rearrange("(p t) b f -> p t (b f)", t=NODE_TILES)
        agg_view = agg.rearrange("d b (p t) f -> d p (b t) f", t=NODE_TILES)
        out_view = out.rearrange("(p t) b f -> p t (b f)", t=NODE_TILES)
        whh_view = whh.rearrange("(g f m) k -> f m g k", g=3, f=FEAT_TILES)
        wih_view = wih.rearrange("(g f m) k -> f m g k", g=3, f=FEAT_TILES)

        def chunk_tiles(c):
            return slice(c * CHUNK_TILES, (c + 1) * CHUNK_TILES)

        def load_x(c):
            nc.sync.dma_start(out=x_nat[:, chunk_tiles(c), :], in_=x_view[:, chunk_tiles(c), :])

        def load_agg(d, c):
            nc.sync.dma_start(out=agg_nat[:, d, chunk_tiles(c), :], in_=agg_view[d][:, chunk_tiles(c), :])

        def load_weights(f):
            nc.sync.dma_start(out=w_nat[:, f, HH_R : HH_N + 1, :], in_=whh_view[f])
            nc.sync.dma_start(out=w_nat[:, f, IH_R : IH_N + 1, :], in_=wih_view[f])

        zeros = keep.tile([P, CHUNK], BF16)
        nc.vector.memset(zeros[:], 0.0)
        warm = keep.tile([P, 1], F32)
        nc.vector.memset(warm[:], 0.0)
        nc.vector.memset(bias_rows[:], 0.0)
        nc.scalar.activation(out=warm[:], in_=warm[:], func=ACT.Sigmoid)
        nc.scalar.dma_start(out=bias_rows[BIH_R:BHH_R, :], in_=bih.rearrange("(r m) -> r m", m=P))
        nc.scalar.dma_start(out=bias_rows[BHH_R:BH, :], in_=bhh.rearrange("(r m) -> r m", m=P))
        nc.scalar.dma_start(out=bias_rows[BH : BH + FEAT_TILES, :], in_=bh.rearrange("(r m) -> r m", m=P))
        half = CHUNK_TILES // 2
        for tiles in (slice(0, half), slice(half, CHUNK_TILES)):
            nc.sync.dma_start(out=x_nat[:, tiles, :], in_=x_view[:, tiles, :])
        nc.sync.dma_start(out=w_nat[:, 0, HH_R : HH_N + 1, :], in_=whh_view[0])
        for tiles in (slice(0, half), slice(half, CHUNK_TILES)):
            nc.sync.dma_start(out=agg_nat[:, 0, tiles, :], in_=agg_view[0][:, tiles, :])
        nc.sync.dma_start(out=w_nat[:, 0, IH_R, :], in_=wih_view[0][:, 0, :])
        nc.sync.dma_start(out=w_nat[:, 0, IH_Z : IH_N + 1, :], in_=wih_view[0][:, 1:, :])
        load_agg(1, 0)
        load_agg(2, 0)
        nc.sync.dma_start(
            out=wh_nat[:].rearrange("p (u e) o -> p u (e o)", u=2),
            in_=wh.rearrange("(u p e) o -> p u (e o)", u=2, e=2),
        )
        for f in range(1, FEAT_TILES):
            load_weights(f)
        load_x(1)
        for d in range(DIRS):
            load_agg(d, 1)

        x_codes = keep.tile([P, NODES], U32, align_bytes=64)
        x_scales = keep.tile([P, NODES], U8, align_bytes=64)
        agg_codes = keep.tile([P, DIRS, NODES], U32, align_bytes=64)
        agg_scales = keep.tile([P, DIRS, NODES], U8, align_bytes=64)
        w_codes = keep.tile([P, FEAT_TILES, 6, P], U32, align_bytes=64)
        w_scales = keep.tile([P, FEAT_TILES, 6, P], U8, align_bytes=64)
        wh_codes = keep.tile([P, FEATS], U32, align_bytes=64)
        wh_scales = keep.tile([P, FEATS], U8, align_bytes=64)

        ident = keep.tile([P, P], F32)
        make_identity(nc, ident[:])

        def node_units(nat, codes, scales, c):
            units = []
            for t in range(c * CHUNK_TILES, (c + 1) * CHUNK_TILES, 2):
                cols = slice(t * P, (t + 2) * P)
                units.append((nat[:, t : t + 2, :], codes[:, cols], scales[:, cols]))
            return units

        def weight_units(f):
            units = []
            for g in range(0, 6, 2):
                units.append(
                    (
                        w_nat[:, f, g : g + 2, :],
                        w_codes[:, f, g : g + 2, :].rearrange("p i m -> p (i m)"),
                        w_scales[:, f, g : g + 2, :].rearrange("p i m -> p (i m)"),
                    )
                )
            return units

        def flip(unit, tag="node", bufs=3):
            words = unit[0].bitcast(F32)
            flipped = psum.tile([P, 2, 2, P], F32, tag=tag, bufs=bufs)
            for i in range(2):
                for u in range(2):
                    nc.tensor.transpose(flipped[:, i, u, :], words[:, i, u * P : (u + 1) * P], ident[:])
            return flipped

        def regroup(flipped, copy):
            grouped = work.tile([P, 2, P, PACK], BF16, align_bytes=64, tag="grouped", bufs=6)
            copy(out=grouped[:].bitcast(F32), in_=flipped[:].rearrange("p i u r -> p i r u"))
            return grouped

        def quantise(unit, grouped):
            nc.vector.quantize_mx(
                out=unit[1].bitcast(FP8X4), scales=unit[2], in_=grouped[:].rearrange("p i r t -> p (i r t)")
            )

        hid_n = {}
        acc_r = {}
        acc_z = {}
        acc_n = {}
        hw_acc = {}
        hw = {}
        reset = {}
        fresh = {}
        fresh_two = {}
        pre = {}
        cand = {}
        part = {}
        fresh_sum = {}
        part_sum = {}
        hw_nodes = {}
        minus_zh = {}
        hsum = {}
        minus_skip = {}
        gated = {}

        def weight_pass(acc, f, g, moving, start, stop):
            nc.tensor.matmul_mx(
                out=acc[:],
                lhsT=w_codes[:, f, g, :].bitcast(FP8X4),
                lhsT_scale=w_scales[:, f, g, :],
                rhs=moving[0].bitcast(FP8X4),
                rhs_scale=moving[1],
                start=start,
                stop=stop,
            )

        def operands(s):
            b, d = divmod(s, DIRS)
            c, f = divmod(b, FEAT_TILES)
            nodes = slice(c * CHUNK, (c + 1) * CHUNK)
            return b, d, f, (x_codes[:, nodes], x_scales[:, nodes]), (agg_codes[:, d, nodes], agg_scales[:, d, nodes])

        def product_r(s):
            b, d, f, xq, aq = operands(s)
            a_r = psum.tile([P, CHUNK], F32, tag="gate", bufs=4)
            weight_pass(a_r, f, IH_R, aq, True, False)
            weight_pass(a_r, f, HH_R, xq, False, True)
            acc_r[s] = a_r

        def product_z(s):
            b, d, f, xq, aq = operands(s)
            a_z = psum.tile([P, CHUNK], F32, tag="gate", bufs=4)
            weight_pass(a_z, f, IH_Z, aq, True, False)
            weight_pass(a_z, f, HH_Z, xq, False, True)
            acc_z[s] = a_z

        def product_n(s):
            b, d, f, xq, aq = operands(s)
            a_n = psum.tile([P, CHUNK], F32, tag="gate", bufs=4)
            weight_pass(a_n, f, IH_N, aq, True, True)
            acc_n[s] = a_n

        def product_hn(b):
            f = b % FEAT_TILES
            h_n = psum.tile([P, CHUNK], F32, tag="hn", bufs=1)
            weight_pass(h_n, f, HH_N, operands(b * DIRS)[3], True, True)
            hid_n[b] = h_n

        def copy_wh(b):
            if b < FEAT_TILES:
                cols = slice(b * P, (b + 1) * P)
                nc.vector.tensor_copy(out=wh_grouped[:, cols, :], in_=wh_nat[:, :, cols].rearrange("p t o -> p o t"))

        def quantise_wh(b):
            if b < FEAT_TILES:
                cols = slice(b * P, (b + 1) * P)
                nc.vector.quantize_mx(
                    out=wh_codes[:, cols].bitcast(FP8X4), scales=wh_scales[:, cols],
                    in_=wh_grouped[:, cols, :].rearrange("p o t -> p (o t)"),
                )

        wh_grouped = keep.tile([P, FEATS, PACK], BF16, align_bytes=64)

        def product_hw(b):
            b, d, f, xq, aq = operands(b * DIRS)
            feats = slice(f * P, (f + 1) * P)
            a_hw = psum.tile([P, CHUNK], F32, tag="gate", bufs=4)
            nc.tensor.matmul_mx(
                out=a_hw[:], lhsT=wh_codes[:, feats].bitcast(FP8X4), lhsT_scale=wh_scales[:, feats],
                rhs=xq[0].bitcast(FP8X4), rhs_scale=xq[1], start=True, stop=True,
            )
            hw_acc[b] = a_hw

        def gate_r(s):
            f = s // DIRS % FEAT_TILES
            r = work.tile([P, CHUNK], F32, tag="reset", bufs=3)
            nc.scalar.activation(out=r[:], in_=acc_r[s][:], func=ACT.Sigmoid, bias=b_r[:, f : f + 1])
            reset[s] = r

        def gate_z(s):
            f = s // DIRS % FEAT_TILES
            fr = work.tile([P, CHUNK], F32, tag="fresh", bufs=9)
            nc.scalar.activation(
                out=fr[:], in_=acc_z[s][:], func=ACT.Sigmoid, bias=minus_b_z[:, f : f + 1], scale=-1.0
            )
            fresh[s] = fr

        def gate_hw(b):
            f = b % FEAT_TILES
            t = work.tile([P, CHUNK], F32, tag="hw", bufs=3)
            nc.scalar.activation(out=t[:], in_=hw_acc[b][:], func=ACT.Relu, bias=bias_cols[:, BH + f : BH + f + 1])
            hw[b] = t

        def pieces(s):
            return [slice(0, CHUNK // 2), slice(CHUNK // 2, CHUNK)] if s == STEPS - 1 else [slice(0, CHUNK)]

        def reset_hidden(s):
            b = s // DIRS
            f = b % FEAT_TILES
            a = work.tile([P, CHUNK], F32, tag="pre", bufs=3)
            for cols in pieces(s):
                nc.vector.scalar_tensor_tensor(
                    out=a[:, cols], in0=hid_n[b][:, cols], scalar=bias_cols[:, BHH_N + f : BHH_N + f + 1],
                    in1=reset[s][:, cols], op0=ALU.add, op1=ALU.mult,
                )
            pre[s] = a

        def candidate_input(s):
            a = pre[s]
            for cols in pieces(s):
                nc.vector.tensor_tensor(out=a[:, cols], in0=acc_n[s][:, cols], in1=a[:, cols], op=ALU.add)

        def candidate(s):
            f = s // DIRS % FEAT_TILES
            cd = work.tile([P, CHUNK], F32, tag="cand", bufs=3)
            for cols in pieces(s):
                nc.scalar.activation(
                    out=cd[:, cols], in_=pre[s][:, cols], func=ACT.Tanh, bias=bias_cols[:, BIH_N + f : BIH_N + f + 1]
                )
            cand[s] = cd

        def blend(s):
            pt = work.tile([P, CHUNK], F32, tag="part", bufs=9)
            engine = nc.vector if s == STEPS - 1 else nc.gpsimd
            for cols in pieces(s):
                engine.tensor_tensor(out=pt[:, cols], in0=fresh[s][:, cols], in1=cand[s][:, cols], op=ALU.mult)
            part[s] = pt

        def add_fresh(s):
            t = work.tile([P, CHUNK], F32, tag="fresh_two")
            nc.gpsimd.tensor_tensor(out=t[:], in0=fresh[s - 1][:], in1=fresh[s][:], op=ALU.add)
            fresh_two[s // DIRS] = t

        def back_to_nodes(terms, tag="node", bufs=3):
            total = psum.tile([P, CHUNK], F32, tag=tag, bufs=bufs)
            for j in range(CHUNK_TILES):
                cols = slice(j * P, (j + 1) * P)
                for i, term in enumerate(terms):
                    nc.tensor.matmul(
                        out=total[:, cols], lhsT=term[:, cols], rhs=ident[:], is_transpose=True,
                        start=(i == 0), stop=(i == len(terms) - 1),
                    )
            return total

        def turn_fresh(b):
            last = b * DIRS + DIRS - 1
            fresh_sum[b] = back_to_nodes([fresh_two[b], fresh[last]])

        def turn_part(b, *bank):
            part_sum[b] = back_to_nodes([part[b * DIRS + d] for d in range(DIRS)], *bank)

        def turn_hw(b, *bank):
            hw_nodes[b] = back_to_nodes([hw[b]], *bank)

        def by_tile(t):
            return t[:].rearrange("p (j m) -> p j m", j=CHUNK_TILES)

        def place(b):
            c, f = divmod(b, FEAT_TILES)
            return chunk_tiles(c), slice(f * P, (f + 1) * P)

        def x_of(b):
            tiles, feats = place(b)
            return x_nat[:, tiles, feats]

        def finish_zh(b):
            t = work.tile([P, CHUNK], F32, tag="minus_zh")
            nc.vector.scalar_tensor_tensor(
                out=by_tile(t), in0=by_tile(fresh_sum[b]), scalar=float(DIRS), in1=x_of(b),
                op0=ALU.subtract, op1=ALU.mult,
            )
            minus_zh[b] = t

        def finish_sum(b):
            t = work.tile([P, CHUNK], F32, tag="hsum")
            for cols in pieces(b * DIRS + DIRS - 1):
                nc.vector.tensor_tensor(
                    out=t[:, cols], in0=part_sum[b][:, cols], in1=minus_zh[b][:, cols], op=ALU.subtract
                )
            hsum[b] = t

        def finish_skip(b):
            t = work.tile([P, CHUNK], F32, tag="minus_skip", bufs=3)
            nc.vector.scalar_tensor_tensor(
                out=by_tile(t), in0=by_tile(hw_nodes[b]), scalar=1.0, in1=x_of(b), op0=ALU.subtract, op1=ALU.mult
            )
            minus_skip[b] = t

        def finish_gate(b):
            t = work.tile([P, CHUNK], F32, tag="gated", bufs=3)
            for cols in pieces(b * DIRS + DIRS - 1):
                nc.vector.scalar_tensor_tensor(
                    out=t[:, cols], in0=hsum[b][:, cols], scalar=0.0, in1=hw_nodes[b][:, cols],
                    op0=ALU.max, op1=ALU.mult,
                )
            gated[b] = t

        def finish_out(b, engine=nc.vector, queue=nc.sync):
            tiles, feats = place(b)
            result = work.tile([P, CHUNK], F32, tag="result", bufs=3)
            for cols in pieces(b * DIRS + DIRS - 1):
                engine.tensor_tensor(
                    out=result[:, cols], in0=gated[b][:, cols], in1=minus_skip[b][:, cols], op=ALU.subtract
                )
                some = slice(tiles.start + cols.start // P, tiles.start + cols.stop // P)
                queue.dma_start(
                    out=out_view[:, some, feats], in_=result[:, cols].rearrange("p (j m) -> p j m", m=P)
                )

        bias_rows32 = keep.tile([P, P], F32)

        def bias_columns():
            bias_flipped = psum.tile([P, P], F32, tag="node", bufs=3)
            nc.tensor.transpose(bias_flipped[:], bias_rows32[:], ident[:])
            nc.vector.tensor_copy(out=bias_cols[:], in_=bias_flipped[:, 0:32])
            nc.vector.tensor_tensor(
                out=b_r[:], in0=bias_cols[:, BIH_R : BIH_R + FEAT_TILES],
                in1=bias_cols[:, BHH_R : BHH_R + FEAT_TILES], op=ALU.add,
            )
            nc.vector.scalar_tensor_tensor(
                out=minus_b_z[:], in0=bias_cols[:, BIH_Z : BIH_Z + FEAT_TILES], scalar=-1.0,
                in1=bias_cols[:, BHH_Z : BHH_Z + FEAT_TILES], op0=ALU.mult, op1=ALU.subtract,
            )

        bias_cols = keep.tile([P, 32], F32)
        b_r = keep.tile([P, FEAT_TILES], F32)
        minus_b_z = keep.tile([P, FEAT_TILES], F32)

        first = node_units(x_nat, x_codes, x_scales, 0)
        weights = weight_units(0)
        first.append(weights[0])
        first.extend(node_units(agg_nat[:, 0], agg_codes[:, 0], agg_scales[:, 0], 0))
        first.extend(weights[1:])
        def keep_busy(count):
            idle = psum.tile([P, CHUNK], F32, tag="hn", bufs=1)
            for n in range(count):
                nc.tensor.matmul(out=idle[:], lhsT=zeros[:, 0:P], rhs=zeros[:], start=True, stop=True)

        keep_busy(4)
        waiting = []
        for i, unit in enumerate(first):
            if i in (2, 3, 5, 6):
                keep_busy(2)
            flipped = flip(unit, "gate", 4) if i < 4 else flip(unit)
            waiting.append((unit, regroup(flipped, nc.vector.tensor_copy if i in (1, 4) else nc.scalar.copy)))
            if len(waiting) > 1:
                quantise(*waiting.pop(0))
            if i == 2:
                nc.scalar.copy(out=bias_rows32[:], in_=bias_rows[:])
            if i == 5:
                bias_columns()
        quantise(*waiting.pop(0))
        keep_busy(1)

        units = []
        for d in range(1, DIRS):
            units.extend(node_units(agg_nat[:, d], agg_codes[:, d], agg_scales[:, d], 0))
        for f in range(1, FEAT_TILES):
            units.extend(weight_units(f))
        units.extend(node_units(x_nat, x_codes, x_scales, 1))
        for d in range(DIRS):
            units.extend(node_units(agg_nat[:, d], agg_codes[:, d], agg_scales[:, d], 1))

        def share(i):
            if i == 0:
                return 3
            return 0 if i > 0 and i % DIRS == 1 else 2

        def ending(j):
            return j // DIRS if 0 <= j < STEPS and j % DIRS == DIRS - 1 else None

        def step(stage, s):
            if 0 <= s < STEPS:
                stage(s)

        def block(stage, s):
            if 0 <= s < STEPS and s % DIRS == DIRS - 1:
                stage(s // DIRS)

        copied = []
        for i in range(-2, STEPS - 1):
            step(product_r, i + 1)
            block(product_hn, i + 3)
            step(product_z, i + 1)
            step(product_n, i + 1)
            block(product_hw, i + 1)
            job = [units.pop(0) for n in range(min(share(i), len(units)))]
            flipped = [flip(unit) for unit in job]
            step(reset_hidden, i)
            step(gate_r, i + 1)
            step(gate_z, i + 1)
            if i < STEPS - 2:
                block(gate_hw, i + 1)
            block(finish_zh, i - 2)
            block(finish_sum, i - 3)
            block(finish_gate, i - 4)
            step(candidate_input, i)
            step(candidate, i)
            step(blend, i)
            if (i + 1) % DIRS == 1:
                step(add_fresh, i + 1)
            copying = [(unit, regroup(fl, nc.scalar.copy)) for unit, fl in zip(job, flipped)]
            block(finish_skip, i - 3)
            block(turn_fresh, i - 1)
            block(turn_part, i - 2)
            block(turn_hw, i - 2)
            for unit, grouped in copied:
                quantise(unit, grouped)
            copied = copying
            block(copy_wh, i + 3)
            block(quantise_wh, i + 2)
            if i < STEPS - 2:
                block(finish_out, i - 5)

        last = STEPS - 1
        before, end = BLOCKS - 2, BLOCKS - 1
        reset_hidden(last)
        candidate_input(last)
        gate_hw(end)
        candidate(last)
        finish_out(end - 2, nc.gpsimd, nc.scalar)
        turn_hw(end, "gate", 4)
        keep_busy(2)
        turn_fresh(end)
        keep_busy(2)
        finish_sum(before)
        finish_skip(before)
        blend(last)
        turn_part(end, "gate", 4)
        finish_gate(before)
        finish_out(before, nc.gpsimd, nc.scalar)
        finish_zh(end)
        finish_skip(end)
        finish_sum(end)
        finish_gate(end)
        finish_out(end)
